import numpy as np
import ml_dtypes


def mxq(x, axis, fmt="e4m3"):
    dtype, down = {"e4m3": (ml_dtypes.float8_e4m3fn, 7), "e5m2": (ml_dtypes.float8_e5m2, 14)}[fmt]
    v = np.moveaxis(np.asarray(x, np.float32).astype(ml_dtypes.bfloat16).astype(np.float64), axis, -1)
    blocks = v.reshape(v.shape[:-1] + (-1, 32))
    amax = np.abs(blocks).max(-1, keepdims=True)
    byte = np.maximum(np.where(amax > 0, np.frexp(amax)[1] - 1 + 127, 0) - down, 1)
    scale = np.exp2(byte - 127.0)
    codes = (blocks / scale).astype(np.float32).astype(dtype).astype(np.float64)
    return np.moveaxis((codes * scale).reshape(v.shape), -1, axis)


WIDE = False


def mx_kscale(k):
    if not WIDE:
        return np.ones(k)
    levels = np.array([10, -10, 5, -5, 0])
    a = np.random.permutation(np.resize(levels, k // 512 * 4)).reshape(k // 512, 4)
    idx = np.arange(k)
    return np.exp2(a[idx // 512, idx % 128 // 32])


BF16 = ml_dtypes.bfloat16


def bf(x):
    return np.asarray(x, np.float32).astype(BF16)


def f64(x):
    return np.asarray(x).astype(np.float64)


E2M1 = np.array([0.0, 0.5, 1.0, 1.5, 2.0, 3.0, 4.0, 6.0, -0.0, -0.5, -1.0, -1.5, -2.0, -3.0, -4.0, -6.0])


def pack_weight(w, fmt):
    k, n = w.shape
    w = f64(bf(w)).reshape(k // 32, 32, n)
    amax = np.abs(w).max(1)
    if fmt == "e4m3":
        byte = np.frexp(amax)[1] - 1 + 127 - 7
    else:
        mant, ex = np.frexp(amax / 6.0)
        byte = np.where(mant > 0.5, ex, ex - 1) + 127
    byte = np.clip(np.where(amax > 0, byte, 1), 1, 254)
    scaled = (w * np.exp2(127.0 - byte)[:, None, :]).reshape(k, n).astype(np.float32)
    by_word = np.ascontiguousarray(scaled.reshape(k // 512, 128, 4, n).transpose(0, 1, 3, 2))
    if fmt == "e4m3":
        words = by_word.astype(ml_dtypes.float8_e4m3fn).view(np.uint8)
    else:
        c = by_word.astype(ml_dtypes.float4_e2m1fn).view(np.uint8) & 0xF
        words = c[..., 0::2] | (c[..., 1::2] << 4)
    return np.ascontiguousarray(words), np.ascontiguousarray(byte.astype(np.uint8).reshape(k // 512, 16, n))


def unpack_weight(words, scales, fmt):
    g, p, n, _ = words.shape
    if fmt == "e4m3":
        vals = np.ascontiguousarray(words).view(ml_dtypes.float8_e4m3fn).astype(np.float64)
    else:
        nib = np.empty((g, p, n, 4), np.uint8)
        nib[..., 0::2] = words & 0xF
        nib[..., 1::2] = words >> 4
        vals = E2M1[nib]
    vals = vals * np.repeat(np.exp2(scales.astype(np.float64) - 127.0), 8, axis=1)[..., None]
    return vals.transpose(0, 1, 3, 2).reshape(g * 512, n)

def pack4(w):
    words, scales = pack_weight(w, "e2m1")
    return words.reshape(words.shape[0], 128, -1), scales


def unpack4(words, scales):
    return unpack_weight(words.reshape(words.shape[0], 128, -1, 2), scales, "e2m1")


B, C, H, W = 2, 512, 32, 32
OFFSETS = [(-1, 0), (1, 0), (0, -1), (0, 1), (-1, -1), (-1, 1), (1, -1), (1, 1)]


def _neighbor_mean(x):
    p = np.pad(x, ((0, 0), (0, 0), (1, 1), (1, 1)), mode="edge")
    h, w = x.shape[2], x.shape[3]
    s = None
    for dy, dx in OFFSETS:
        sl = p[:, :, 1 + dy:1 + dy + h, 1 + dx:1 + dx + w]
        s = sl if s is None else s + sl
    return s / 8.0


def setup_inputs():
    s = mx_kscale(C)
    s = s / s.max()
    x = bf(np.random.standard_normal((B, C, H, W)) * s[None, :, None, None])
    wp = np.random.standard_normal((C, 2 * C)) / np.sqrt(C) / np.concatenate([s, s])[None, :]
    words, scales = pack4(np.ascontiguousarray(wp.T))
    b = bf(np.random.standard_normal(C) * 0.3)
    return {"x": x, "Wp_words": words, "Wp_scales": scales, "b": b}


def reference(x, Wp_words, Wp_scales, b):
    x, b = f64(x), f64(b)
    wt = unpack4(Wp_words, Wp_scales)
    n, c, h, w = x.shape
    mean = _neighbor_mean(x)
    xq = mxq(x, 1, "e4m3").reshape(n, c, h * w)
    mq = mxq(mean, 1, "e4m3").reshape(n, c, h * w)
    out = ((wt[:c].T @ xq)
           + (wt[c:].T @ mq)).reshape(n, c, h, w) + b[None, :, None, None]
    return np.maximum(out, 0.0) + x

@@ -1,0 +1,223 @@
+from contextlib import ExitStack
+
+import concourse.mybir as mybir
+from concourse.masks import make_identity
+
+FLOPS = 2 * 2 * 1024 * 512 * 1024
+
+BF16 = mybir.dt.bfloat16
+F32 = mybir.dt.float32
+I32 = mybir.dt.int32
+U8 = mybir.dt.uint8
+U32 = mybir.dt.uint32
+FP8X4 = mybir.dt.float8_e4m3fn_x4
+FP4X4 = mybir.dt.float4_e2m1fn_x4
+ADD = mybir.AluOpType.add
+RELU = mybir.ActivationFunctionType.Relu
+
+P = 128
+T = 4
+SIDE = 32
+HW = SIDE * SIDE
+ROW = SIDE * T
+CH = 512
+
+
+def tile_staticgraphmodule_kernel(tc, x, Wp_words, Wp_scales, b, out):
+    nc = tc.nc
+    with ExitStack() as ctx:
+        keep = ctx.enter_context(tc.tile_pool(name="keep", bufs=1))
+        ypool = ctx.enter_context(tc.tile_pool(name="ypool", bufs=4))
+        psum = ctx.enter_context(tc.psum_pool(name="psum", bufs=8))
+        ctx.enter_context(tc.manual_schedule())
+
+        x_pj = [x[n].rearrange("(p j) h w -> p j (h w)", j=T) for n in range(2)]
+        x_mp = [x[n].rearrange("(m p) h w -> p m (h w)", p=P) for n in range(2)]
+        out_mp = [out[n].rearrange("(m p) h w -> p m (h w)", p=P) for n in range(2)]
+        xraw = [keep.tile([P, T, HW], BF16, name="xraw%d" % n) for n in range(2)]
+        xres = [keep.tile([P, T, HW], BF16, name="xres%d" % n) for n in range(2)]
+        for half in range(2):
+            cs = slice(CH * half, CH * (half + 1))
+            for n in (1, 0):
+                nc.sync.dma_start(out=xraw[n][:, :, cs], in_=x_pj[n][:, :, cs])
+        ww = keep.tile([P, 2, 1024], U8, name="ww", align_bytes=64)
+        nc.sync.dma_start(out=ww[:].bitcast(I32), in_=Wp_words.rearrange("g p c -> p g c").bitcast(I32))
+        wsc = keep.tile([P, 2, 512], U8, name="wsc", align_bytes=64)
+        nc.vector.memset(wsc[:].bitcast(I32), 0)
+        for q in range(4):
+            nc.sync.dma_start(
+                out=wsc[32 * q:32 * q + 4, :, :].bitcast(I32),
+                in_=Wp_scales[:, 4 * q:4 * q + 4, :].rearrange("g r n -> r g n").bitcast(I32),
+            )
+        brow = keep.tile([P, P], BF16, name="brow")
+        nc.vector.memset(brow[:].bitcast(I32), 0)
+        nc.sync.dma_start(out=brow[0:4, :], in_=b.rearrange("(m p) -> m p", p=P))
+        for n in range(2):
+            nc.sync.dma_start(out=xres[n][:], in_=x_mp[n])
+
+        z = keep.tile([P, 8 * SIDE], BF16, name="z")
+        nc.gpsimd.memset(z[:], 0.0)
+        make_identity(nc, z[:, 64:192], nomemset=True)
+        ident = z[:, 64:192]
+        z8 = keep.tile([P, 8, SIDE], BF16, name="z8")
+        hz = keep.tile([P, 8, SIDE], BF16, name="hz")
+        rz = keep.tile([P, 8, SIDE], BF16, name="rz")
+        vz = keep.tile([P, 6, SIDE], BF16, name="vz")
+        a_int = keep.tile([P, 6, SIDE], BF16, name="a_int")
+        a_top = keep.tile([P, P], BF16, name="a_top")
+        a_bot = keep.tile([P, P], BF16, name="a_bot")
+        nc.vector.tensor_scalar_mul(out=z8[:], in0=z[:].rearrange("p (r w) -> p r w", w=SIDE), scalar1=0.125)
+        nc.vector.tensor_tensor(out=hz[:, :, 1:31], in0=z8[:, :, 0:30], in1=z8[:, :, 2:32], op=ADD)
+        nc.vector.tensor_tensor(out=hz[:, :, 0:32:31], in0=z8[:, :, 0:31:30], in1=z8[:, :, 1:32:30], op=ADD)
+        nc.vector.tensor_tensor(out=rz[:], in0=hz[:], in1=z8[:], op=ADD)
+        nc.vector.tensor_tensor(out=vz[:], in0=rz[:, 0:6, :], in1=rz[:, 2:8, :], op=ADD)
+        nc.vector.tensor_tensor(out=a_int[:], in0=vz[:], in1=hz[:, 1:7, :], op=ADD)
+        af = a_int[:].rearrange("p r w -> p (r w)")
+        nc.vector.tensor_copy(out=a_top[:, 32:128], in_=af[:, 64:160])
+        nc.vector.tensor_tensor(out=a_top[:, 0:32], in0=af[:, 32:64], in1=af[:, 0:32], op=ADD)
+        nc.vector.tensor_copy(out=a_bot[:, 0:96], in_=af[:, 32:128])
+        nc.vector.tensor_tensor(out=a_bot[:, 96:128], in0=af[:, 128:160], in1=af[:, 160:192], op=ADD)
+
+        bias = keep.tile([P, 4], F32, name="bias")
+        xg = [keep.tile([P, HW, T], BF16, name="xg%d" % n, align_bytes=64) for n in range(2)]
+        gm = [keep.tile([P, HW, T], BF16, name="gm%d" % n, align_bytes=64) for n in range(2)]
+        xc = [keep.tile([P, HW], U32, name="xc%d" % n, align_bytes=64) for n in range(2)]
+        mc = [keep.tile([P, HW], U32, name="mc%d" % n, align_bytes=64) for n in range(2)]
+        xs = [keep.tile([P, HW], U8, name="xs%d" % n, align_bytes=64) for n in range(2)]
+        ms = [keep.tile([P, HW], U8, name="ms%d" % n, align_bytes=64) for n in range(2)]
+        xt = keep.tile([P, 8, T, P], BF16, name="xt")
+        x8 = keep.tile([P, HW, T], BF16, name="x8")
+        hh = keep.tile([P, SIDE, ROW], F32, name="hh")
+        rr = keep.tile([P, SIDE, ROW], F32, name="rr")
+        vv = keep.tile([P, SIDE, ROW], F32, name="vv")
+        xr = x8[:].rearrange("p (i j) t -> p i (j t)", j=SIDE)
+        x4 = x8[:].rearrange("p (i j) t -> p i j t", j=SIDE)
+        h4 = hh[:].rearrange("p i (j t) -> p i j t", t=T)
+        g1 = gm[1][:].rearrange("p (i j) t -> p i (j t)", j=SIDE)
+        ys = {}
+
+        def regroup_x(n, c):
+            cs = slice(CH * c, CH * (c + 1))
+            nc.scalar.copy(
+                out=xg[n][:, cs, :].rearrange("p (c i) t -> p c t i", i=4),
+                in_=xraw[n][:, :, cs].rearrange("p t (c i) -> p c t i", i=4),
+            )
+
+        def quantise(src, codes, plane, c):
+            cs = slice(CH * c, CH * (c + 1))
+            nc.vector.quantize_mx(
+                out=codes[:, cs].bitcast(FP8X4),
+                scales=plane[:, cs],
+                in_=src[:, cs, :].rearrange("p w t -> p (w t)"),
+            )
+
+        def quantise_both(n, c):
+            quantise(xg[n], xc[n], xs[n], c)
+            quantise(gm[n], mc[n], ms[n], c)
+
+        def project(n, c):
+            cs = slice(CH * c, CH * (c + 1))
+            y = ypool.tile([P, 4, CH], F32, tag="y", name="y%d%d" % (n, c))
+            ys[(n, c)] = y
+            for m in range(4):
+                acc = psum.tile([P, CH], F32, tag="bank", name="acc")
+                for g, codes, plane in ((0, xc[n], xs[n]), (1, mc[n], ms[n])):
+                    nc.tensor.matmul_mx(
+                        out=acc[:],
+                        lhsT=ww[:, g, 256 * m:256 * (m + 1)].bitcast(FP4X4),
+                        lhsT_scale=wsc[:, g, P * m:P * (m + 1)],
+                        rhs=codes[:, cs].bitcast(FP8X4),
+                        rhs_scale=plane[:, cs],
+                        start=(g == 0),
+                        stop=(g == 1),
+                    )
+                nc.scalar.activation(out=y[:, m, :], in_=acc[:], func=RELU, bias=bias[:, m:m + 1], scale=1.0)
+
+        def finish(n, c, m0, m1):
+            cs = slice(CH * c, CH * (c + 1))
+            y = ys[(n, c)]
+            nc.vector.tensor_tensor(out=y[:, m0:m1, :], in0=y[:, m0:m1, :], in1=xres[n][:, m0:m1, cs], op=ADD)
+            nc.sync.dma_start(out=out_mp[n][:, m0:m1, cs], in_=y[:, m0:m1, :])
+
+        def transposes(pair):
+            pt = psum.tile([P, 8, P], BF16, tag="bank", name="pt")
+            for s in range(8):
+                kb = 2 * pair + s // 4
+                nc.tensor.transpose(pt[:, s, :], xraw[0][:, s % 4, P * kb:P * (kb + 1)], ident)
+            nc.scalar.copy(out=xt[:, 2 * pair:2 * pair + 2, :, :].rearrange("p k t c -> p (k t) c"), in_=pt[:])
+
+        def band(ob):
+            pm = psum.tile([P, T, P], F32, tag="bank", name="pm")
+            main = a_top[:] if ob == 0 else (a_bot[:] if ob == 7 else af[:, 32:160])
+            for t in range(T):
+                nc.tensor.matmul(out=pm[:, t, :], lhsT=xt[:, ob, t, :], rhs=main, start=True, stop=False)
+                if ob > 0:
+                    nc.tensor.matmul(out=pm[:, t, 0:32], lhsT=xt[:, ob - 1, t, :], rhs=af[:, 160:192], start=False, stop=(ob == 7))
+                if ob < 7:
+                    nc.tensor.matmul(out=pm[:, t, 96:128], lhsT=xt[:, ob + 1, t, :], rhs=af[:, 0:32], start=False, stop=True)
+            nc.scalar.copy(out=gm[0][:, P * ob:P * (ob + 1), :], in_=pm[:].rearrange("p t w -> p w t"))
+
+        def eighth(c):
+            cs = slice(CH * c, CH * (c + 1))
+            nc.vector.tensor_scalar_mul(
+                out=x8[:, cs, :].rearrange("p (c i) t -> p c t i", i=4),
+                in0=xraw[1][:, :, cs].rearrange("p t (c i) -> p c t i", i=4),
+                scalar1=0.125,
+            )
+
+        def vadd(o, a, c):
+            nc.vector.tensor_tensor(out=o, in0=a, in1=c, op=ADD)
+
+        def row_sums(r0, r1):
+            mid = (r0 + r1) // 2
+            vadd(h4[:, r0:r1, 0:32:31, :], x4[:, r0:r1, 0:31:30, :], x4[:, r0:r1, 1:32:30, :])
+            for a, e in ((r0, mid), (mid, r1)):
+                vadd(hh[:, a:e, T:ROW - T], xr[:, a:e, 0:ROW - 2 * T], xr[:, a:e, 2 * T:ROW])
+            for a, e in ((r0, mid), (mid, r1)):
+                vadd(rr[:, a:e, :], hh[:, a:e, :], xr[:, a:e, :])
+
+        def col_sums(r0, r1, mid):
+            if r0 == 0:
+                vadd(vv[:, 0:1, :], rr[:, 0:1, :], rr[:, 1:2, :])
+            for a, e in ((max(r0, 1), mid - 1), (mid - 1, min(r1, SIDE - 1))):
+                vadd(vv[:, a:e, :], rr[:, a - 1:e - 1, :], rr[:, a + 1:e + 1, :])
+            if r1 == SIDE:
+                vadd(vv[:, 31:32, :], rr[:, 30:31, :], rr[:, 31:32, :])
+            for a, e in ((r0, mid - 1), (mid - 1, r1)):
+                vadd(g1[:, a:e, :], vv[:, a:e, :], hh[:, a:e, :])
+
+        transposes(0)
+        transposes(1)
+        eighth(0)
+        eighth(1)
+        regroup_x(0, 0)
+        transposes(2)
+        transposes(3)
+        pb = psum.tile([P, 8, P], BF16, tag="bank", name="pb")
+        nc.tensor.transpose(pb[:, 0, :], brow[:], ident)
+        nc.scalar.copy(out=bias[:], in_=pb[:, 0, 0:4])
+        row_sums(0, 17)
+        col_sums(0, 16, 8)
+        for ob in range(4):
+            band(ob)
+        regroup_x(1, 0)
+        regroup_x(0, 1)
+        for ob in range(4, 8):
+            band(ob)
+        quantise_both(0, 0)
+        quantise_both(1, 0)
+        project(0, 0)
+        project(1, 0)
+        row_sums(17, 32)
+        quantise_both(0, 1)
+        project(0, 1)
+        finish(0, 0, 0, 4)
+        finish(1, 0, 0, 4)
+        finish(0, 1, 0, 2)
+        regroup_x(1, 1)
+        col_sums(16, 32, 24)
+        quantise_both(1, 1)
+        project(1, 1)
+        finish(0, 1, 2, 4)
+        for m in range(4):
+            finish(1, 1, m, m + 1)

@@ -21,12 +21,14 @@ SIDE = 32
 HW = SIDE * SIDE
 ROW = SIDE * T
 CH = 512
+VROWS = 17
 
 
 def tile_staticgraphmodule_kernel(tc, x, Wp_words, Wp_scales, b, out):
     nc = tc.nc
     with ExitStack() as ctx:
         keep = ctx.enter_context(tc.tile_pool(name="keep", bufs=1))
+        xtpool = ctx.enter_context(tc.tile_pool(name="xtpool", bufs=4))
         ypool = ctx.enter_context(tc.tile_pool(name="ypool", bufs=4))
         psum = ctx.enter_context(tc.psum_pool(name="psum", bufs=8))
         ctx.enter_context(tc.manual_schedule())
@@ -36,10 +38,8 @@ def tile_staticgraphmodule_kernel(tc, x, Wp_words, Wp_scales, b, out):
         out_mp = [out[n].rearrange("(m p) h w -> p m (h w)", p=P) for n in range(2)]
         xraw = [keep.tile([P, T, HW], BF16, name="xraw%d" % n) for n in range(2)]
         xres = [keep.tile([P, T, HW], BF16, name="xres%d" % n) for n in range(2)]
-        for half in range(2):
-            cs = slice(CH * half, CH * (half + 1))
-            for n in (1, 0):
-                nc.sync.dma_start(out=xraw[n][:, :, cs], in_=x_pj[n][:, :, cs])
+        for n, r0, r1 in ((0, 0, 17), (1, 15, 32), (0, 17, 32), (1, 0, 15)):
+            nc.sync.dma_start(out=xraw[n][:, :, SIDE * r0:SIDE * r1], in_=x_pj[n][:, :, SIDE * r0:SIDE * r1])
         ww = keep.tile([P, 2, 1024], U8, name="ww", align_bytes=64)
         nc.sync.dma_start(out=ww[:].bitcast(I32), in_=Wp_words.rearrange("g p c -> p g c").bitcast(I32))
         wsc = keep.tile([P, 2, 512], U8, name="wsc", align_bytes=64)
@@ -55,6 +55,9 @@ def tile_staticgraphmodule_kernel(tc, x, Wp_words, Wp_scales, b, out):
         for n in range(2):
             nc.sync.dma_start(out=xres[n][:], in_=x_mp[n])
 
+        def vadd(o, a, c):
+            nc.vector.tensor_tensor(out=o, in0=a, in1=c, op=ADD)
+
         z = keep.tile([P, 8 * SIDE], BF16, name="z")
         nc.gpsimd.memset(z[:], 0.0)
         make_identity(nc, z[:, 64:192], nomemset=True)
@@ -64,19 +67,19 @@ def tile_staticgraphmodule_kernel(tc, x, Wp_words, Wp_scales, b, out):
         rz = keep.tile([P, 8, SIDE], BF16, name="rz")
         vz = keep.tile([P, 6, SIDE], BF16, name="vz")
         a_int = keep.tile([P, 6, SIDE], BF16, name="a_int")
-        a_top = keep.tile([P, P], BF16, name="a_top")
-        a_bot = keep.tile([P, P], BF16, name="a_bot")
+        a_first = keep.tile([P, 2 * SIDE], BF16, name="a_first")
+        a_last = keep.tile([P, 2 * SIDE], BF16, name="a_last")
         nc.vector.tensor_scalar_mul(out=z8[:], in0=z[:].rearrange("p (r w) -> p r w", w=SIDE), scalar1=0.125)
-        nc.vector.tensor_tensor(out=hz[:, :, 1:31], in0=z8[:, :, 0:30], in1=z8[:, :, 2:32], op=ADD)
-        nc.vector.tensor_tensor(out=hz[:, :, 0:32:31], in0=z8[:, :, 0:31:30], in1=z8[:, :, 1:32:30], op=ADD)
-        nc.vector.tensor_tensor(out=rz[:], in0=hz[:], in1=z8[:], op=ADD)
-        nc.vector.tensor_tensor(out=vz[:], in0=rz[:, 0:6, :], in1=rz[:, 2:8, :], op=ADD)
-        nc.vector.tensor_tensor(out=a_int[:], in0=vz[:], in1=hz[:, 1:7, :], op=ADD)
+        vadd(hz[:, :, 1:31], z8[:, :, 0:30], z8[:, :, 2:32])
+        vadd(hz[:, :, 0:32:31], z8[:, :, 0:31:30], z8[:, :, 1:32:30])
+        vadd(rz[:], hz[:], z8[:])
+        vadd(vz[:], rz[:, 0:6, :], rz[:, 2:8, :])
+        vadd(a_int[:], vz[:], hz[:, 1:7, :])
         af = a_int[:].rearrange("p r w -> p (r w)")
-        nc.vector.tensor_copy(out=a_top[:, 32:128], in_=af[:, 64:160])
-        nc.vector.tensor_tensor(out=a_top[:, 0:32], in0=af[:, 32:64], in1=af[:, 0:32], op=ADD)
-        nc.vector.tensor_copy(out=a_bot[:, 0:96], in_=af[:, 32:128])
-        nc.vector.tensor_tensor(out=a_bot[:, 96:128], in0=af[:, 128:160], in1=af[:, 160:192], op=ADD)
+        vadd(a_first[:, 0:32], af[:, 32:64], af[:, 0:32])
+        nc.vector.tensor_copy(out=a_first[:, 32:64], in_=af[:, 64:96])
+        nc.vector.tensor_copy(out=a_last[:, 0:32], in_=af[:, 96:128])
+        vadd(a_last[:, 32:64], af[:, 128:160], af[:, 160:192])
 
         bias = keep.tile([P, 4], F32, name="bias")
         xg = [keep.tile([P, HW, T], BF16, name="xg%d" % n, align_bytes=64) for n in range(2)]
@@ -85,23 +88,25 @@ def tile_staticgraphmodule_kernel(tc, x, Wp_words, Wp_scales, b, out):
         mc = [keep.tile([P, HW], U32, name="mc%d" % n, align_bytes=64) for n in range(2)]
         xs = [keep.tile([P, HW], U8, name="xs%d" % n, align_bytes=64) for n in range(2)]
         ms = [keep.tile([P, HW], U8, name="ms%d" % n, align_bytes=64) for n in range(2)]
-        xt = keep.tile([P, 8, T, P], BF16, name="xt")
-        x8 = keep.tile([P, HW, T], BF16, name="x8")
-        hh = keep.tile([P, SIDE, ROW], F32, name="hh")
-        rr = keep.tile([P, SIDE, ROW], F32, name="rr")
-        vv = keep.tile([P, SIDE, ROW], F32, name="vv")
+        x8 = keep.tile([P, VROWS * SIDE, T], BF16, name="x8")
+        hh = keep.tile([P, VROWS, ROW], F32, name="hh")
+        rr = keep.tile([P, VROWS, ROW], F32, name="rr")
+        vv = keep.tile([P, VROWS, ROW], F32, name="vv")
         xr = x8[:].rearrange("p (i j) t -> p i (j t)", j=SIDE)
         x4 = x8[:].rearrange("p (i j) t -> p i j t", j=SIDE)
         h4 = hh[:].rearrange("p i (j t) -> p i j t", t=T)
-        g1 = gm[1][:].rearrange("p (i j) t -> p i (j t)", j=SIDE)
+        g1 = gm[1][:, CH:HW, :].rearrange("p (i j) t -> p i (j t)", j=SIDE)
+        xts = {}
         ys = {}
 
-        def regroup_x(n, c):
+        def regroup_x(engine, n, c):
             cs = slice(CH * c, CH * (c + 1))
-            nc.scalar.copy(
-                out=xg[n][:, cs, :].rearrange("p (c i) t -> p c t i", i=4),
-                in_=xraw[n][:, :, cs].rearrange("p t (c i) -> p c t i", i=4),
-            )
+            dst = xg[n][:, cs, :].rearrange("p (c i) t -> p c t i", i=4)
+            src = xraw[n][:, :, cs].rearrange("p t (c i) -> p c t i", i=4)
+            if engine == "vector":
+                nc.vector.tensor_copy(out=dst, in_=src)
+            else:
+                nc.scalar.copy(out=dst, in_=src)
 
         def quantise(src, codes, plane, c):
             cs = slice(CH * c, CH * (c + 1))
@@ -136,88 +141,84 @@ def tile_staticgraphmodule_kernel(tc, x, Wp_words, Wp_scales, b, out):
         def finish(n, c, m0, m1):
             cs = slice(CH * c, CH * (c + 1))
             y = ys[(n, c)]
-            nc.vector.tensor_tensor(out=y[:, m0:m1, :], in0=y[:, m0:m1, :], in1=xres[n][:, m0:m1, cs], op=ADD)
+            vadd(y[:, m0:m1, :], y[:, m0:m1, :], xres[n][:, m0:m1, cs])
             nc.sync.dma_start(out=out_mp[n][:, m0:m1, cs], in_=y[:, m0:m1, :])
 
-        def transposes(pair):
+        def flip(n, c, i):
             pt = psum.tile([P, 8, P], BF16, tag="bank", name="pt")
-            for s in range(8):
-                kb = 2 * pair + s // 4
-                nc.tensor.transpose(pt[:, s, :], xraw[0][:, s % 4, P * kb:P * (kb + 1)], ident)
-            nc.scalar.copy(out=xt[:, 2 * pair:2 * pair + 2, :, :].rearrange("p k t c -> p (k t) c"), in_=pt[:])
+            for wi in range(2):
+                first = min(max(16 * c + 4 * i + 2 * wi - 1, 0), SIDE - 4)
+                for t in range(T):
+                    nc.tensor.transpose(pt[:, T * wi + t, :], xraw[n][:, t, SIDE * first:SIDE * first + P], ident)
+            xt = xtpool.tile([P, 8, P], BF16, tag="xt", name="xt")
+            xts[(n, c, i)] = xt
+            nc.scalar.copy(out=xt[:], in_=pt[:])
 
-        def band(ob):
+        def mean_pe(n, c, i):
             pm = psum.tile([P, T, P], F32, tag="bank", name="pm")
-            main = a_top[:] if ob == 0 else (a_bot[:] if ob == 7 else af[:, 32:160])
-            for t in range(T):
-                nc.tensor.matmul(out=pm[:, t, :], lhsT=xt[:, ob, t, :], rhs=main, start=True, stop=False)
-                if ob > 0:
-                    nc.tensor.matmul(out=pm[:, t, 0:32], lhsT=xt[:, ob - 1, t, :], rhs=af[:, 160:192], start=False, stop=(ob == 7))
-                if ob < 7:
-                    nc.tensor.matmul(out=pm[:, t, 96:128], lhsT=xt[:, ob + 1, t, :], rhs=af[:, 0:32], start=False, stop=True)
-            nc.scalar.copy(out=gm[0][:, P * ob:P * (ob + 1), :], in_=pm[:].rearrange("p t w -> p w t"))
+            xt = xts[(n, c, i)]
+            for wi in range(2):
+                a = 16 * c + 4 * i + 2 * wi
+                band = a_first[:] if a == 0 else (a_last[:] if a == SIDE - 2 else af[:, 64:128])
+                for t in range(T):
+                    nc.tensor.matmul(out=pm[:, t, 64 * wi:64 * (wi + 1)], lhsT=xt[:, T * wi + t, :], rhs=band, start=True, stop=True)
+            w0 = CH * c + P * i
+            nc.scalar.copy(out=gm[n][:, w0:w0 + P, :], in_=pm[:].rearrange("p t w -> p w t"))
 
-        def eighth(c):
-            cs = slice(CH * c, CH * (c + 1))
+        def mean_chunk(n, c):
+            flip(n, c, 0)
+            for i in range(1, 4):
+                flip(n, c, i)
+                mean_pe(n, c, i - 1)
+            mean_pe(n, c, 3)
+
+        def eighth():
             nc.vector.tensor_scalar_mul(
-                out=x8[:, cs, :].rearrange("p (c i) t -> p c t i", i=4),
-                in0=xraw[1][:, :, cs].rearrange("p t (c i) -> p c t i", i=4),
+                out=x8[:].rearrange("p (c i) t -> p c t i", i=4),
+                in0=xraw[1][:, :, SIDE * (SIDE - VROWS):HW].rearrange("p t (c i) -> p c t i", i=4),
                 scalar1=0.125,
             )
 
-        def vadd(o, a, c):
-            nc.vector.tensor_tensor(out=o, in0=a, in1=c, op=ADD)
-
-        def row_sums(r0, r1):
-            mid = (r0 + r1) // 2
-            vadd(h4[:, r0:r1, 0:32:31, :], x4[:, r0:r1, 0:31:30, :], x4[:, r0:r1, 1:32:30, :])
-            for a, e in ((r0, mid), (mid, r1)):
+        def row_sums():
+            vadd(h4[:, :, 0:32:31, :], x4[:, :, 0:31:30, :], x4[:, :, 1:32:30, :])
+            for a, e in ((0, 8), (8, VROWS)):
                 vadd(hh[:, a:e, T:ROW - T], xr[:, a:e, 0:ROW - 2 * T], xr[:, a:e, 2 * T:ROW])
-            for a, e in ((r0, mid), (mid, r1)):
+            for a, e in ((0, 8), (8, VROWS)):
                 vadd(rr[:, a:e, :], hh[:, a:e, :], xr[:, a:e, :])
 
-        def col_sums(r0, r1, mid):
-            if r0 == 0:
-                vadd(vv[:, 0:1, :], rr[:, 0:1, :], rr[:, 1:2, :])
-            for a, e in ((max(r0, 1), mid - 1), (mid - 1, min(r1, SIDE - 1))):
+        def col_sums():
+            for a, e in ((1, 7), (7, VROWS - 1)):
                 vadd(vv[:, a:e, :], rr[:, a - 1:e - 1, :], rr[:, a + 1:e + 1, :])
-            if r1 == SIDE:
-                vadd(vv[:, 31:32, :], rr[:, 30:31, :], rr[:, 31:32, :])
-            for a, e in ((r0, mid - 1), (mid - 1, r1)):
-                vadd(g1[:, a:e, :], vv[:, a:e, :], hh[:, a:e, :])
+            vadd(vv[:, VROWS - 1:VROWS, :], rr[:, VROWS - 2:VROWS - 1, :], rr[:, VROWS - 1:VROWS, :])
+            for a, e in ((1, 7), (7, VROWS)):
+                vadd(g1[:, a - 1:e - 1, :], vv[:, a:e, :], hh[:, a:e, :])
 
-        transposes(0)
-        transposes(1)
-        eighth(0)
-        eighth(1)
-        regroup_x(0, 0)
-        transposes(2)
-        transposes(3)
-        pb = psum.tile([P, 8, P], BF16, tag="bank", name="pb")
-        nc.tensor.transpose(pb[:, 0, :], brow[:], ident)
-        nc.scalar.copy(out=bias[:], in_=pb[:, 0, 0:4])
-        row_sums(0, 17)
-        col_sums(0, 16, 8)
-        for ob in range(4):
-            band(ob)
-        regroup_x(1, 0)
-        regroup_x(0, 1)
-        for ob in range(4, 8):
-            band(ob)
+        def load_bias():
+            pb = psum.tile([P, 8, P], BF16, tag="bank", name="pb")
+            nc.tensor.transpose(pb[:, 0, :], brow[:], ident)
+            nc.scalar.copy(out=bias[:], in_=pb[:, 0, 0:4])
+
+        regroup_x("vector", 0, 0)
+        mean_chunk(0, 0)
+        eighth()
+        row_sums()
         quantise_both(0, 0)
-        quantise_both(1, 0)
+        mean_chunk(0, 1)
+        load_bias()
         project(0, 0)
-        project(1, 0)
-        row_sums(17, 32)
+        regroup_x("vector", 0, 1)
+        col_sums()
         quantise_both(0, 1)
+        mean_chunk(1, 0)
         project(0, 1)
-        finish(0, 0, 0, 4)
-        finish(1, 0, 0, 4)
-        finish(0, 1, 0, 2)
-        regroup_x(1, 1)
-        col_sums(16, 32, 24)
+        regroup_x("vector", 1, 1)
         quantise_both(1, 1)
         project(1, 1)
-        finish(0, 1, 2, 4)
+        finish(0, 0, 0, 4)
+        regroup_x("vector", 1, 0)
+        quantise_both(1, 0)
+        project(1, 0)
+        finish(0, 1, 0, 4)
+        finish(1, 1, 0, 4)
         for m in range(4):
-            finish(1, 1, m, m + 1)
+            finish(1, 0, m, m + 1)

@@ -13,7 +13,8 @@ U32 = mybir.dt.uint32
 FP8X4 = mybir.dt.float8_e4m3fn_x4
 FP4X4 = mybir.dt.float4_e2m1fn_x4
 ADD = mybir.AluOpType.add
-RELU = mybir.ActivationFunctionType.Relu
+MAX = mybir.AluOpType.max
+IDENTITY = mybir.ActivationFunctionType.Identity
 
 P = 128
 T = 4
@@ -21,7 +22,8 @@ SIDE = 32
 HW = SIDE * SIDE
 ROW = SIDE * T
 CH = 512
-VROWS = 17
+PE_ROWS = (32, 19)
+V0 = PE_ROWS[1] - 16
 
 
 def tile_staticgraphmodule_kernel(tc, x, Wp_words, Wp_scales, b, out):
@@ -29,7 +31,6 @@ def tile_staticgraphmodule_kernel(tc, x, Wp_words, Wp_scales, b, out):
     with ExitStack() as ctx:
         keep = ctx.enter_context(tc.tile_pool(name="keep", bufs=1))
         xtpool = ctx.enter_context(tc.tile_pool(name="xtpool", bufs=4))
-        ypool = ctx.enter_context(tc.tile_pool(name="ypool", bufs=4))
         psum = ctx.enter_context(tc.psum_pool(name="psum", bufs=8))
         ctx.enter_context(tc.manual_schedule())
 
@@ -38,7 +39,7 @@ def tile_staticgraphmodule_kernel(tc, x, Wp_words, Wp_scales, b, out):
         out_mp = [out[n].rearrange("(m p) h w -> p m (h w)", p=P) for n in range(2)]
         xraw = [keep.tile([P, T, HW], BF16, name="xraw%d" % n) for n in range(2)]
         xres = [keep.tile([P, T, HW], BF16, name="xres%d" % n) for n in range(2)]
-        for n, r0, r1 in ((0, 0, 17), (1, 15, 32), (0, 17, 32), (1, 0, 15)):
+        for n, r0, r1 in ((0, 0, 17), (1, 16, 32), (0, 17, 32), (1, 0, 16)):
             nc.sync.dma_start(out=xraw[n][:, :, SIDE * r0:SIDE * r1], in_=x_pj[n][:, :, SIDE * r0:SIDE * r1])
         ww = keep.tile([P, 2, 1024], U8, name="ww", align_bytes=64)
         nc.sync.dma_start(out=ww[:].bitcast(I32), in_=Wp_words.rearrange("g p c -> p g c").bitcast(I32))
@@ -82,31 +83,29 @@ def tile_staticgraphmodule_kernel(tc, x, Wp_words, Wp_scales, b, out):
         vadd(a_last[:, 32:64], af[:, 128:160], af[:, 160:192])
 
         bias = keep.tile([P, 4], F32, name="bias")
+        negb = keep.tile([P, 4], F32, name="negb")
+        xb = [keep.tile([P, 4, HW], F32, name="xb%d" % n) for n in range(2)]
         xg = [keep.tile([P, HW, T], BF16, name="xg%d" % n, align_bytes=64) for n in range(2)]
         gm = [keep.tile([P, HW, T], BF16, name="gm%d" % n, align_bytes=64) for n in range(2)]
         xc = [keep.tile([P, HW], U32, name="xc%d" % n, align_bytes=64) for n in range(2)]
         mc = [keep.tile([P, HW], U32, name="mc%d" % n, align_bytes=64) for n in range(2)]
         xs = [keep.tile([P, HW], U8, name="xs%d" % n, align_bytes=64) for n in range(2)]
         ms = [keep.tile([P, HW], U8, name="ms%d" % n, align_bytes=64) for n in range(2)]
-        x8 = keep.tile([P, VROWS * SIDE, T], BF16, name="x8")
-        hh = keep.tile([P, VROWS, ROW], F32, name="hh")
-        rr = keep.tile([P, VROWS, ROW], F32, name="rr")
-        vv = keep.tile([P, VROWS, ROW], F32, name="vv")
-        xr = x8[:].rearrange("p (i j) t -> p i (j t)", j=SIDE)
-        x4 = x8[:].rearrange("p (i j) t -> p i j t", j=SIDE)
+        x8 = keep.tile([P, 16, ROW], BF16, name="x8")
+        hh = keep.tile([P, 16, ROW], F32, name="hh")
+        rr = keep.tile([P, 16, ROW], F32, name="rr")
+        vv = keep.tile([P, 16, ROW], F32, name="vv")
+        x4 = x8[:].rearrange("p i (j t) -> p i j t", t=T)
         h4 = hh[:].rearrange("p i (j t) -> p i j t", t=T)
         g1 = gm[1][:, CH:HW, :].rearrange("p (i j) t -> p i (j t)", j=SIDE)
         xts = {}
-        ys = {}
 
-        def regroup_x(engine, n, c):
+        def regroup_x(n, c):
             cs = slice(CH * c, CH * (c + 1))
-            dst = xg[n][:, cs, :].rearrange("p (c i) t -> p c t i", i=4)
-            src = xraw[n][:, :, cs].rearrange("p t (c i) -> p c t i", i=4)
-            if engine == "vector":
-                nc.vector.tensor_copy(out=dst, in_=src)
-            else:
-                nc.scalar.copy(out=dst, in_=src)
+            nc.vector.tensor_copy(
+                out=xg[n][:, cs, :].rearrange("p (c i) t -> p c t i", i=4),
+                in_=xraw[n][:, :, cs].rearrange("p t (c i) -> p c t i", i=4),
+            )
 
         def quantise(src, codes, plane, c):
             cs = slice(CH * c, CH * (c + 1))
@@ -116,109 +115,87 @@ def tile_staticgraphmodule_kernel(tc, x, Wp_words, Wp_scales, b, out):
                 in_=src[:, cs, :].rearrange("p w t -> p (w t)"),
             )
 
-        def quantise_both(n, c):
-            quantise(xg[n], xc[n], xs[n], c)
-            quantise(gm[n], mc[n], ms[n], c)
+        def windows(n, a0):
+            return [(a, min(2, PE_ROWS[n] - a)) for a in (a0, a0 + 2) if a < PE_ROWS[n]]
 
-        def project(n, c):
-            cs = slice(CH * c, CH * (c + 1))
-            y = ypool.tile([P, 4, CH], F32, tag="y", name="y%d%d" % (n, c))
-            ys[(n, c)] = y
-            for m in range(4):
-                acc = psum.tile([P, CH], F32, tag="bank", name="acc")
-                for g, codes, plane in ((0, xc[n], xs[n]), (1, mc[n], ms[n])):
-                    nc.tensor.matmul_mx(
-                        out=acc[:],
-                        lhsT=ww[:, g, 256 * m:256 * (m + 1)].bitcast(FP4X4),
-                        lhsT_scale=wsc[:, g, P * m:P * (m + 1)],
-                        rhs=codes[:, cs].bitcast(FP8X4),
-                        rhs_scale=plane[:, cs],
-                        start=(g == 0),
-                        stop=(g == 1),
-                    )
-                nc.scalar.activation(out=y[:, m, :], in_=acc[:], func=RELU, bias=bias[:, m:m + 1], scale=1.0)
-
-        def finish(n, c, m0, m1):
-            cs = slice(CH * c, CH * (c + 1))
-            y = ys[(n, c)]
-            vadd(y[:, m0:m1, :], y[:, m0:m1, :], xres[n][:, m0:m1, cs])
-            nc.sync.dma_start(out=out_mp[n][:, m0:m1, cs], in_=y[:, m0:m1, :])
-
-        def flip(n, c, i):
+        def flip(n, a0):
             pt = psum.tile([P, 8, P], BF16, tag="bank", name="pt")
-            for wi in range(2):
-                first = min(max(16 * c + 4 * i + 2 * wi - 1, 0), SIDE - 4)
+            for wi, (a, rows) in enumerate(windows(n, a0)):
+                first = min(max(a - 1, 0), SIDE - 4)
                 for t in range(T):
                     nc.tensor.transpose(pt[:, T * wi + t, :], xraw[n][:, t, SIDE * first:SIDE * first + P], ident)
             xt = xtpool.tile([P, 8, P], BF16, tag="xt", name="xt")
-            xts[(n, c, i)] = xt
+            xts[(n, a0)] = xt
             nc.scalar.copy(out=xt[:], in_=pt[:])
 
-        def mean_pe(n, c, i):
+        def mean_pe(n, a0):
             pm = psum.tile([P, T, P], F32, tag="bank", name="pm")
-            xt = xts[(n, c, i)]
-            for wi in range(2):
-                a = 16 * c + 4 * i + 2 * wi
+            xt = xts[(n, a0)]
+            done = 0
+            for wi, (a, rows) in enumerate(windows(n, a0)):
                 band = a_first[:] if a == 0 else (a_last[:] if a == SIDE - 2 else af[:, 64:128])
                 for t in range(T):
-                    nc.tensor.matmul(out=pm[:, t, 64 * wi:64 * (wi + 1)], lhsT=xt[:, T * wi + t, :], rhs=band, start=True, stop=True)
-            w0 = CH * c + P * i
-            nc.scalar.copy(out=gm[n][:, w0:w0 + P, :], in_=pm[:].rearrange("p t w -> p w t"))
+                    nc.tensor.matmul(
+                        out=pm[:, t, 64 * wi:64 * wi + SIDE * rows], lhsT=xt[:, T * wi + t, :], rhs=band[:, 0:SIDE * rows],
+                        start=True, stop=True,
+                    )
+                done += SIDE * rows
+            nc.scalar.copy(out=gm[n][:, SIDE * a0:SIDE * a0 + done, :], in_=pm[:, :, 0:done].rearrange("p t w -> p w t"))
 
-        def mean_chunk(n, c):
-            flip(n, c, 0)
-            for i in range(1, 4):
-                flip(n, c, i)
-                mean_pe(n, c, i - 1)
-            mean_pe(n, c, 3)
+        regroup_x(0, 0)
+        regroup_x(1, 1)
+        lo = V0 - 1
+        nc.vector.tensor_scalar_mul(
+            out=x8[:, lo:16, :], in0=xg[1][:, CH + SIDE * lo:HW, :].rearrange("p (i j) t -> p i (j t)", j=SIDE), scalar1=0.125
+        )
+        mid = (lo + 16) // 2
+        vadd(h4[:, lo:16, 0:32:31, :], x4[:, lo:16, 0:31:30, :], x4[:, lo:16, 1:32:30, :])
+        for a, e in ((lo, mid), (mid, 16)):
+            vadd(hh[:, a:e, T:ROW - T], x8[:, a:e, 0:ROW - 2 * T], x8[:, a:e, 2 * T:ROW])
+        for a, e in ((lo, mid), (mid, 16)):
+            vadd(rr[:, a:e, :], hh[:, a:e, :], x8[:, a:e, :])
+        for a, e in ((V0, mid - 1), (mid - 1, 15)):
+            vadd(vv[:, a:e, :], rr[:, a - 1:e - 1, :], rr[:, a + 1:e + 1, :])
+        vadd(vv[:, 15:16, :], rr[:, 14:15, :], rr[:, 15:16, :])
+        for a, e in ((V0, mid - 1), (mid - 1, 16)):
+            vadd(g1[:, a:e, :], vv[:, a:e, :], hh[:, a:e, :])
+        regroup_x(0, 1)
+        regroup_x(1, 0)
 
-        def eighth():
-            nc.vector.tensor_scalar_mul(
-                out=x8[:].rearrange("p (c i) t -> p c t i", i=4),
-                in0=xraw[1][:, :, SIDE * (SIDE - VROWS):HW].rearrange("p t (c i) -> p c t i", i=4),
-                scalar1=0.125,
-            )
+        banks = [(n, a0) for n in range(2) for a0 in range(0, PE_ROWS[n], 4)]
+        flip(*banks[0])
+        for i in range(1, len(banks)):
+            flip(*banks[i])
+            mean_pe(*banks[i - 1])
+        mean_pe(*banks[-1])
+        pb = psum.tile([P, 8, P], BF16, tag="bank", name="pb")
+        nc.tensor.transpose(pb[:, 0, :], brow[:], ident)
+        nc.scalar.copy(out=bias[:], in_=pb[:, 0, 0:4])
+        nc.scalar.mul(out=negb[:], in_=pb[:, 0, 0:4], mul=-1.0)
 
-        def row_sums():
-            vadd(h4[:, :, 0:32:31, :], x4[:, :, 0:31:30, :], x4[:, :, 1:32:30, :])
-            for a, e in ((0, 8), (8, VROWS)):
-                vadd(hh[:, a:e, T:ROW - T], xr[:, a:e, 0:ROW - 2 * T], xr[:, a:e, 2 * T:ROW])
-            for a, e in ((0, 8), (8, VROWS)):
-                vadd(rr[:, a:e, :], hh[:, a:e, :], xr[:, a:e, :])
+        for n in range(2):
+            for c in range(2):
+                quantise(xg[n], xc[n], xs[n], c)
+        for n, c in ((0, 0), (0, 1), (1, 0), (1, 1)):
+            quantise(gm[n], mc[n], ms[n], c)
 
-        def col_sums():
-            for a, e in ((1, 7), (7, VROWS - 1)):
-                vadd(vv[:, a:e, :], rr[:, a - 1:e - 1, :], rr[:, a + 1:e + 1, :])
-            vadd(vv[:, VROWS - 1:VROWS, :], rr[:, VROWS - 2:VROWS - 1, :], rr[:, VROWS - 1:VROWS, :])
-            for a, e in ((1, 7), (7, VROWS)):
-                vadd(g1[:, a - 1:e - 1, :], vv[:, a:e, :], hh[:, a:e, :])
-
-        def load_bias():
-            pb = psum.tile([P, 8, P], BF16, tag="bank", name="pb")
-            nc.tensor.transpose(pb[:, 0, :], brow[:], ident)
-            nc.scalar.copy(out=bias[:], in_=pb[:, 0, 0:4])
-
-        regroup_x("vector", 0, 0)
-        mean_chunk(0, 0)
-        eighth()
-        row_sums()
-        quantise_both(0, 0)
-        mean_chunk(0, 1)
-        load_bias()
-        project(0, 0)
-        regroup_x("vector", 0, 1)
-        col_sums()
-        quantise_both(0, 1)
-        mean_chunk(1, 0)
-        project(0, 1)
-        regroup_x("vector", 1, 1)
-        quantise_both(1, 1)
-        project(1, 1)
-        finish(0, 0, 0, 4)
-        regroup_x("vector", 1, 0)
-        quantise_both(1, 0)
-        project(1, 0)
-        finish(0, 1, 0, 4)
-        finish(1, 1, 0, 4)
-        for m in range(4):
-            finish(1, 0, m, m + 1)
+        for n in range(2):
+            for m in range(4):
+                nc.scalar.activation(out=xb[n][:, m, :], in_=xres[n][:, m, :], func=IDENTITY, bias=bias[:, m:m + 1], scale=1.0)
+                for c in range(2):
+                    cs = slice(CH * c, CH * (c + 1))
+                    acc = psum.tile([P, CH], F32, tag="bank", name="acc")
+                    for g, codes, plane in ((0, xc[n], xs[n]), (1, mc[n], ms[n])):
+                        nc.tensor.matmul_mx(
+                            out=acc[:],
+                            lhsT=ww[:, g, 256 * m:256 * (m + 1)].bitcast(FP4X4),
+                            lhsT_scale=wsc[:, g, P * m:P * (m + 1)],
+                            rhs=codes[:, cs].bitcast(FP8X4),
+                            rhs_scale=plane[:, cs],
+                            start=(g == 0),
+                            stop=(g == 1),
+                        )
+                    nc.vector.scalar_tensor_tensor(
+                        out=xb[n][:, m, cs], in0=acc[:], scalar=negb[:, m:m + 1], in1=xb[n][:, m, cs], op0=MAX, op1=ADD
+                    )
+                    nc.sync.dma_start(out=out_mp[n][:, m, cs], in_=xb[n][:, m, cs])

@@ -102,10 +102,7 @@ def tile_staticgraphmodule_kernel(tc, x, Wp_words, Wp_scales, b, out):
 
         def regroup_x(n, c):
             cs = slice(CH * c, CH * (c + 1))
-            nc.vector.tensor_copy(
-                out=xg[n][:, cs, :].rearrange("p (c i) t -> p c t i", i=4),
-                in_=xraw[n][:, :, cs].rearrange("p t (c i) -> p c t i", i=4),
-            )
+            nc.vector.tensor_copy(out=xg[n][:, cs, :], in_=xraw[n][:, :, cs].rearrange("p t w -> p w t"))
 
         def quantise(src, codes, plane, c):
             cs = slice(CH * c, CH * (c + 1))
@@ -126,7 +123,9 @@ def tile_staticgraphmodule_kernel(tc, x, Wp_words, Wp_scales, b, out):
                     nc.tensor.transpose(pt[:, T * wi + t, :], xraw[n][:, t, SIDE * first:SIDE * first + P], ident)
             xt = xtpool.tile([P, 8, P], BF16, tag="xt", name="xt")
             xts[(n, a0)] = xt
-            nc.scalar.copy(out=xt[:], in_=pt[:])
+            nc.scalar.copy(
+                out=xt[:].rearrange("p a b -> p (a b)").bitcast(F32), in_=pt[:].rearrange("p a b -> p (a b)").bitcast(F32)
+            )
 
         def mean_pe(n, a0):
             pm = psum.tile([P, T, P], F32, tag="bank", name="pm")

@@ -39,7 +39,7 @@ def tile_staticgraphmodule_kernel(tc, x, Wp_words, Wp_scales, b, out):
         out_mp = [out[n].rearrange("(m p) h w -> p m (h w)", p=P) for n in range(2)]
         xraw = [keep.tile([P, T, HW], BF16, name="xraw%d" % n) for n in range(2)]
         xres = [keep.tile([P, T, HW], BF16, name="xres%d" % n) for n in range(2)]
-        for n, r0, r1 in ((0, 0, 17), (1, 16, 32), (0, 17, 32), (1, 0, 16)):
+        for n, r0, r1 in ((0, 0, 9), (1, 16, 24), (0, 9, 17), (1, 24, 32), (0, 17, 32), (1, 0, 16)):
             nc.sync.dma_start(out=xraw[n][:, :, SIDE * r0:SIDE * r1], in_=x_pj[n][:, :, SIDE * r0:SIDE * r1])
         ww = keep.tile([P, 2, 1024], U8, name="ww", align_bytes=64)
         nc.sync.dma_start(out=ww[:].bitcast(I32), in_=Wp_words.rearrange("g p c -> p g c").bitcast(I32))
@@ -100,8 +100,8 @@ def tile_staticgraphmodule_kernel(tc, x, Wp_words, Wp_scales, b, out):
         g1 = gm[1][:, CH:HW, :].rearrange("p (i j) t -> p i (j t)", j=SIDE)
         xts = {}
 
-        def regroup_x(n, c):
-            cs = slice(CH * c, CH * (c + 1))
+        def regroup_x(n, c, halves=(0, 1)):
+            cs = slice(CH * c + 256 * halves[0], CH * c + 256 * (halves[-1] + 1))
             nc.vector.tensor_copy(out=xg[n][:, cs, :], in_=xraw[n][:, :, cs].rearrange("p t w -> p w t"))
 
         def quantise(src, codes, plane, c):
@@ -141,25 +141,26 @@ def tile_staticgraphmodule_kernel(tc, x, Wp_words, Wp_scales, b, out):
                 done += SIDE * rows
             nc.scalar.copy(out=gm[n][:, SIDE * a0:SIDE * a0 + done, :], in_=pm[:, :, 0:done].rearrange("p t w -> p w t"))
 
-        regroup_x(0, 0)
-        regroup_x(1, 1)
+        regroup_x(0, 0, (0,))
+        regroup_x(1, 1, (0,))
+        regroup_x(0, 0, (1,))
+        regroup_x(1, 1, (1,))
         lo = V0 - 1
         nc.vector.tensor_scalar_mul(
             out=x8[:, lo:16, :], in0=xg[1][:, CH + SIDE * lo:HW, :].rearrange("p (i j) t -> p i (j t)", j=SIDE), scalar1=0.125
         )
-        mid = (lo + 16) // 2
-        vadd(h4[:, lo:16, 0:32:31, :], x4[:, lo:16, 0:31:30, :], x4[:, lo:16, 1:32:30, :])
-        for a, e in ((lo, mid), (mid, 16)):
-            vadd(hh[:, a:e, T:ROW - T], x8[:, a:e, 0:ROW - 2 * T], x8[:, a:e, 2 * T:ROW])
-        for a, e in ((lo, mid), (mid, 16)):
-            vadd(rr[:, a:e, :], hh[:, a:e, :], x8[:, a:e, :])
-        for a, e in ((V0, mid - 1), (mid - 1, 15)):
-            vadd(vv[:, a:e, :], rr[:, a - 1:e - 1, :], rr[:, a + 1:e + 1, :])
-        vadd(vv[:, 15:16, :], rr[:, 14:15, :], rr[:, 15:16, :])
-        for a, e in ((V0, mid - 1), (mid - 1, 16)):
-            vadd(g1[:, a:e, :], vv[:, a:e, :], hh[:, a:e, :])
         regroup_x(0, 1)
+        vadd(h4[:, lo:16, 0:32:31, :], x4[:, lo:16, 0:31:30, :], x4[:, lo:16, 1:32:30, :])
+        vadd(hh[:, lo:16, T:ROW - T], x8[:, lo:16, 0:ROW - 2 * T], x8[:, lo:16, 2 * T:ROW])
         regroup_x(1, 0)
+        vadd(rr[:, lo:16, :], hh[:, lo:16, :], x8[:, lo:16, :])
+        quantise(xg[0], xc[0], xs[0], 0)
+        vadd(vv[:, V0:15, :], rr[:, V0 - 1:14, :], rr[:, V0 + 1:16, :])
+        vadd(vv[:, 15:16, :], rr[:, 14:15, :], rr[:, 15:16, :])
+        quantise(xg[1], xc[1], xs[1], 1)
+        vadd(g1[:, V0:16, :], vv[:, V0:16, :], hh[:, V0:16, :])
+        quantise(xg[0], xc[0], xs[0], 1)
+        quantise(xg[1], xc[1], xs[1], 0)
 
         banks = [(n, a0) for n in range(2) for a0 in range(0, PE_ROWS[n], 4)]
         flip(*banks[0])
@@ -172,15 +173,16 @@ def tile_staticgraphmodule_kernel(tc, x, Wp_words, Wp_scales, b, out):
         nc.scalar.copy(out=bias[:], in_=pb[:, 0, 0:4])
         nc.scalar.mul(out=negb[:], in_=pb[:, 0, 0:4], mul=-1.0)
 
-        for n in range(2):
-            for c in range(2):
-                quantise(xg[n], xc[n], xs[n], c)
-        for n, c in ((0, 0), (0, 1), (1, 0), (1, 1)):
-            quantise(gm[n], mc[n], ms[n], c)
+        nc.vector.quantize_mx(out=mc[0][:].bitcast(FP8X4), scales=ms[0][:], in_=gm[0][:].rearrange("p w t -> p (w t)"))
+        for c in range(2):
+            quantise(gm[1], mc[1], ms[1], c)
 
         for n in range(2):
             for m in range(4):
-                nc.scalar.activation(out=xb[n][:, m, :], in_=xres[n][:, m, :], func=IDENTITY, bias=bias[:, m:m + 1], scale=1.0)
+                for part in ((slice(0, CH), slice(CH, HW)) if (n, m) == (1, 3) else (slice(0, HW),)):
+                    nc.scalar.activation(
+                        out=xb[n][:, m, part], in_=xres[n][:, m, part], func=IDENTITY, bias=bias[:, m:m + 1], scale=1.0
+                    )
                 for c in range(2):
                     cs = slice(CH * c, CH * (c + 1))
                     acc = psum.tile([P, CH], F32, tag="bank", name="acc")

@@ -14,6 +14,7 @@ FP8X4 = mybir.dt.float8_e4m3fn_x4
 FP4X4 = mybir.dt.float4_e2m1fn_x4
 ADD = mybir.AluOpType.add
 MAX = mybir.AluOpType.max
+MULT = mybir.AluOpType.mult
 IDENTITY = mybir.ActivationFunctionType.Identity
 
 P = 128
@@ -152,15 +153,13 @@ def tile_staticgraphmodule_kernel(tc, x, Wp_words, Wp_scales, b, out):
         regroup_x(0, 1)
         vadd(h4[:, lo:16, 0:32:31, :], x4[:, lo:16, 0:31:30, :], x4[:, lo:16, 1:32:30, :])
         vadd(hh[:, lo:16, T:ROW - T], x8[:, lo:16, 0:ROW - 2 * T], x8[:, lo:16, 2 * T:ROW])
-        regroup_x(1, 0)
-        vadd(rr[:, lo:16, :], hh[:, lo:16, :], x8[:, lo:16, :])
         quantise(xg[0], xc[0], xs[0], 0)
+        vadd(rr[:, lo:16, :], hh[:, lo:16, :], x8[:, lo:16, :])
+        quantise(xg[0], xc[0], xs[0], 1)
         vadd(vv[:, V0:15, :], rr[:, V0 - 1:14, :], rr[:, V0 + 1:16, :])
         vadd(vv[:, 15:16, :], rr[:, 14:15, :], rr[:, 15:16, :])
         quantise(xg[1], xc[1], xs[1], 1)
         vadd(g1[:, V0:16, :], vv[:, V0:16, :], hh[:, V0:16, :])
-        quantise(xg[0], xc[0], xs[0], 1)
-        quantise(xg[1], xc[1], xs[1], 0)
 
         banks = [(n, a0) for n in range(2) for a0 in range(0, PE_ROWS[n], 4)]
         flip(*banks[0])
@@ -176,27 +175,33 @@ def tile_staticgraphmodule_kernel(tc, x, Wp_words, Wp_scales, b, out):
         nc.vector.quantize_mx(out=mc[0][:].bitcast(FP8X4), scales=ms[0][:], in_=gm[0][:].rearrange("p w t -> p (w t)"))
         for c in range(2):
             quantise(gm[1], mc[1], ms[1], c)
+        one = keep.tile([P, 1], F32, name="one")
+        nc.vector.memset(one[:], 1.0)
+        for q in range(4):
+            qs = slice(P * q, P * (q + 1))
+            nc.gpsimd.tensor_scalar(
+                out=xg[1][:, qs, :], in0=xraw[1][:, :, qs].rearrange("p t w -> p w t"), scalar1=one[:, 0:1], scalar2=0.0,
+                op0=MULT, op1=ADD,
+            )
 
-        for n in range(2):
-            for m in range(4):
-                for part in ((slice(0, CH), slice(CH, HW)) if (n, m) == (1, 3) else (slice(0, HW),)):
-                    nc.scalar.activation(
-                        out=xb[n][:, m, part], in_=xres[n][:, m, part], func=IDENTITY, bias=bias[:, m:m + 1], scale=1.0
-                    )
-                for c in range(2):
-                    cs = slice(CH * c, CH * (c + 1))
-                    acc = psum.tile([P, CH], F32, tag="bank", name="acc")
-                    for g, codes, plane in ((0, xc[n], xs[n]), (1, mc[n], ms[n])):
-                        nc.tensor.matmul_mx(
-                            out=acc[:],
-                            lhsT=ww[:, g, 256 * m:256 * (m + 1)].bitcast(FP4X4),
-                            lhsT_scale=wsc[:, g, P * m:P * (m + 1)],
-                            rhs=codes[:, cs].bitcast(FP8X4),
-                            rhs_scale=plane[:, cs],
-                            start=(g == 0),
-                            stop=(g == 1),
-                        )
-                    nc.vector.scalar_tensor_tensor(
-                        out=xb[n][:, m, cs], in0=acc[:], scalar=negb[:, m:m + 1], in1=xb[n][:, m, cs], op0=MAX, op1=ADD
-                    )
-                    nc.sync.dma_start(out=out_mp[n][:, m, cs], in_=xb[n][:, m, cs])
+        tiles = [(0, m, c) for m in range(4) for c in range(2)] + [(1, m, c) for c in (1, 0) for m in range(4)]
+        for i, (n, m, c) in enumerate(tiles):
+            cs = slice(CH * c, CH * (c + 1))
+            nc.scalar.activation(out=xb[n][:, m, cs], in_=xres[n][:, m, cs], func=IDENTITY, bias=bias[:, m:m + 1], scale=1.0)
+            acc = psum.tile([P, CH], F32, tag="bank", name="acc")
+            for g, codes, plane in ((0, xc[n], xs[n]), (1, mc[n], ms[n])):
+                nc.tensor.matmul_mx(
+                    out=acc[:],
+                    lhsT=ww[:, g, 256 * m:256 * (m + 1)].bitcast(FP4X4),
+                    lhsT_scale=wsc[:, g, P * m:P * (m + 1)],
+                    rhs=codes[:, cs].bitcast(FP8X4),
+                    rhs_scale=plane[:, cs],
+                    start=(g == 0),
+                    stop=(g == 1),
+                )
+            nc.vector.scalar_tensor_tensor(
+                out=xb[n][:, m, cs], in0=acc[:], scalar=negb[:, m:m + 1], in1=xb[n][:, m, cs], op0=MAX, op1=ADD
+            )
+            nc.sync.dma_start(out=out_mp[n][:, m, cs], in_=xb[n][:, m, cs])
+            if i == 6:
+                quantise(xg[1], xc[1], xs[1], 0)

@@ -23,7 +23,7 @@ SIDE = 32
 HW = SIDE * SIDE
 ROW = SIDE * T
 CH = 512
-PE_ROWS = (32, 19)
+PE_ROWS = (32, 18)
 V0 = PE_ROWS[1] - 16
 
 
@@ -40,7 +40,7 @@ def tile_staticgraphmodule_kernel(tc, x, Wp_words, Wp_scales, b, out):
         out_mp = [out[n].rearrange("(m p) h w -> p m (h w)", p=P) for n in range(2)]
         xraw = [keep.tile([P, T, HW], BF16, name="xraw%d" % n) for n in range(2)]
         xres = [keep.tile([P, T, HW], BF16, name="xres%d" % n) for n in range(2)]
-        for n, r0, r1 in ((0, 0, 9), (1, 16, 24), (0, 9, 17), (1, 24, 32), (0, 17, 32), (1, 0, 16)):
+        for n, r0, r1 in ((0, 0, 9), (1, 16, 24), (1, 24, 32), (0, 9, 17), (0, 17, 32), (1, 0, 16)):
             nc.sync.dma_start(out=xraw[n][:, :, SIDE * r0:SIDE * r1], in_=x_pj[n][:, :, SIDE * r0:SIDE * r1])
         ww = keep.tile([P, 2, 1024], U8, name="ww", align_bytes=64)
         nc.sync.dma_start(out=ww[:].bitcast(I32), in_=Wp_words.rearrange("g p c -> p g c").bitcast(I32))
@@ -124,8 +124,10 @@ def tile_staticgraphmodule_kernel(tc, x, Wp_words, Wp_scales, b, out):
                     nc.tensor.transpose(pt[:, T * wi + t, :], xraw[n][:, t, SIDE * first:SIDE * first + P], ident)
             xt = xtpool.tile([P, 8, P], BF16, tag="xt", name="xt")
             xts[(n, a0)] = xt
+            used = T * len(windows(n, a0))
             nc.scalar.copy(
-                out=xt[:].rearrange("p a b -> p (a b)").bitcast(F32), in_=pt[:].rearrange("p a b -> p (a b)").bitcast(F32)
+                out=xt[:, 0:used, :].rearrange("p a b -> p (a b)").bitcast(F32),
+                in_=pt[:, 0:used, :].rearrange("p a b -> p (a b)").bitcast(F32),
             )
 
         def mean_pe(n, a0):
@@ -144,8 +146,8 @@ def tile_staticgraphmodule_kernel(tc, x, Wp_words, Wp_scales, b, out):
 
         regroup_x(0, 0, (0,))
         regroup_x(1, 1, (0,))
-        regroup_x(0, 0, (1,))
         regroup_x(1, 1, (1,))
+        regroup_x(0, 0, (1,))
         lo = V0 - 1
         nc.vector.tensor_scalar_mul(
             out=x8[:, lo:16, :], in0=xg[1][:, CH + SIDE * lo:HW, :].rearrange("p (i j) t -> p i (j t)", j=SIDE), scalar1=0.125

@@ -164,6 +164,9 @@ def tile_staticgraphmodule_kernel(tc, x, Wp_words, Wp_scales, b, out):
         vadd(g1[:, V0:16, :], vv[:, V0:16, :], hh[:, V0:16, :])
 
         banks = [(n, a0) for n in range(2) for a0 in range(0, PE_ROWS[n], 4)]
+        idle = psum.tile([P, 8, P], BF16, tag="bank", name="idle")
+        for j in range(8):
+            nc.tensor.transpose(idle[:, j, :], ident, ident)
         flip(*banks[0])
         for i in range(1, len(banks)):
             flip(*banks[i])

@@ -23,7 +23,8 @@ SIDE = 32
 HW = SIDE * SIDE
 ROW = SIDE * T
 CH = 512
-PE_ROWS = (32, 18)
+PE_ROWS = (32, 19)
+AHEAD = 8
 V0 = PE_ROWS[1] - 16
 
 
@@ -54,8 +55,6 @@ def tile_staticgraphmodule_kernel(tc, x, Wp_words, Wp_scales, b, out):
         brow = keep.tile([P, P], BF16, name="brow")
         nc.vector.memset(brow[:].bitcast(I32), 0)
         nc.sync.dma_start(out=brow[0:4, :], in_=b.rearrange("(m p) -> m p", p=P))
-        for n in range(2):
-            nc.sync.dma_start(out=xres[n][:], in_=x_mp[n])
 
         def vadd(o, a, c):
             nc.vector.tensor_tensor(out=o, in0=a, in1=c, op=ADD)
@@ -80,8 +79,8 @@ def tile_staticgraphmodule_kernel(tc, x, Wp_words, Wp_scales, b, out):
         af = a_int[:].rearrange("p r w -> p (r w)")
         vadd(a_first[:, 0:32], af[:, 32:64], af[:, 0:32])
         nc.vector.tensor_copy(out=a_first[:, 32:64], in_=af[:, 64:96])
-        nc.vector.tensor_copy(out=a_last[:, 0:32], in_=af[:, 96:128])
-        vadd(a_last[:, 32:64], af[:, 128:160], af[:, 160:192])
+        mid = af[:, 64:128]
+        a_top = keep.tile([P, 3 * SIDE], BF16, name="a_top")
 
         bias = keep.tile([P, 4], F32, name="bias")
         negb = keep.tile([P, 4], F32, name="negb")
@@ -100,6 +99,8 @@ def tile_staticgraphmodule_kernel(tc, x, Wp_words, Wp_scales, b, out):
         h4 = hh[:].rearrange("p i (j t) -> p i j t", t=T)
         g1 = gm[1][:, CH:HW, :].rearrange("p (i j) t -> p i (j t)", j=SIDE)
         xts = {}
+        at = keep.tile([P, 5, T * P], BF16, name="at")
+        bt = keep.tile([P, 4, T * P], BF16, name="bt")
 
         def regroup_x(n, c, halves=(0, 1)):
             cs = slice(CH * c + 256 * halves[0], CH * c + 256 * (halves[-1] + 1))
@@ -144,26 +145,62 @@ def tile_staticgraphmodule_kernel(tc, x, Wp_words, Wp_scales, b, out):
                 done += SIDE * rows
             nc.scalar.copy(out=gm[n][:, SIDE * a0:SIDE * a0 + done, :], in_=pm[:, :, 0:done].rearrange("p t w -> p w t"))
 
+        def flip1(k0):
+            ks = [k for k in (k0, k0 + 1) if k < 5]
+            pt = psum.tile([P, 8, P], BF16, tag="bank", name="pt1")
+            for i, k in enumerate(ks):
+                for t in range(T):
+                    nc.tensor.transpose(pt[:, T * i + t, :], xraw[1][:, t, P * k:P * (k + 1)], ident)
+            used = T * len(ks)
+            nc.scalar.copy(
+                out=at[:, k0:k0 + len(ks), :].rearrange("p a b -> p (a b)").bitcast(F32),
+                in_=pt[:, 0:used, :].rearrange("p a b -> p (a b)").bitcast(F32),
+            )
+            up = [k for k in ks if k < 4]
+            if up:
+                nc.sync.dma_start(out=bt[0:64, up[0]:up[-1] + 1, :], in_=at[64:128, up[0]:up[-1] + 1, :])
+            low = [k for k in ks if k >= 1]
+            if low:
+                nc.sync.dma_start(out=bt[64:128, low[0] - 1:low[-1], :], in_=at[0:64, low[0]:low[-1] + 1, :])
+
+        def mean1(j):
+            pm = psum.tile([P, T, P], F32, tag="bank", name="pm1")
+            parts = [(at, 0, a_top[:], 96)] if j == 0 else [(bt, j - 1, mid, 64), (at, j, mid, 64)]
+            done = 0
+            for xt, k, band, width in parts:
+                for t in range(T):
+                    nc.tensor.matmul(
+                        out=pm[:, t, done:done + width], lhsT=xt[:, k, P * t:P * (t + 1)], rhs=band[:, 0:width],
+                        start=True, stop=True,
+                    )
+                done += width
+            first = SIDE * max(4 * j - 1, 0)
+            nc.scalar.copy(out=gm[1][:, first:first + done, :], in_=pm[:, :, 0:done].rearrange("p t w -> p w t"))
+
+        lo = V0 - 1
+        x1 = xg[1][:, CH:HW, :].rearrange("p (i j) t -> p i (j t)", j=SIDE)
         regroup_x(0, 0, (0,))
         regroup_x(1, 1, (0,))
         regroup_x(1, 1, (1,))
+        nc.vector.tensor_scalar_mul(out=x8[:, lo:8, :], in0=x1[:, lo:8, :], scalar1=0.125)
+        nc.vector.tensor_scalar_mul(out=x8[:, 8:16, :], in0=x1[:, 8:16, :], scalar1=0.125)
         regroup_x(0, 0, (1,))
-        lo = V0 - 1
-        nc.vector.tensor_scalar_mul(
-            out=x8[:, lo:16, :], in0=xg[1][:, CH + SIDE * lo:HW, :].rearrange("p (i j) t -> p i (j t)", j=SIDE), scalar1=0.125
-        )
-        regroup_x(0, 1)
         vadd(h4[:, lo:16, 0:32:31, :], x4[:, lo:16, 0:31:30, :], x4[:, lo:16, 1:32:30, :])
         vadd(hh[:, lo:16, T:ROW - T], x8[:, lo:16, 0:ROW - 2 * T], x8[:, lo:16, 2 * T:ROW])
-        quantise(xg[0], xc[0], xs[0], 0)
+        nc.vector.tensor_copy(out=a_last[:, 0:32], in_=af[:, 96:128])
+        vadd(a_last[:, 32:64], af[:, 128:160], af[:, 160:192])
+        nc.vector.tensor_copy(out=a_top[:, 0:32], in_=a_first[:, 0:32])
+        nc.vector.tensor_copy(out=a_top[:, 32:96], in_=mid)
+        regroup_x(0, 1)
         vadd(rr[:, lo:16, :], hh[:, lo:16, :], x8[:, lo:16, :])
-        quantise(xg[0], xc[0], xs[0], 1)
+        quantise(xg[0], xc[0], xs[0], 0)
         vadd(vv[:, V0:15, :], rr[:, V0 - 1:14, :], rr[:, V0 + 1:16, :])
         vadd(vv[:, 15:16, :], rr[:, 14:15, :], rr[:, 15:16, :])
-        quantise(xg[1], xc[1], xs[1], 1)
+        quantise(xg[0], xc[0], xs[0], 1)
         vadd(g1[:, V0:16, :], vv[:, V0:16, :], hh[:, V0:16, :])
+        quantise(xg[1], xc[1], xs[1], 1)
 
-        banks = [(n, a0) for n in range(2) for a0 in range(0, PE_ROWS[n], 4)]
+        banks = [(0, a0) for a0 in range(0, PE_ROWS[0], 4)]
         idle = psum.tile([P, 8, P], BF16, tag="bank", name="idle")
         for j in range(8):
             nc.tensor.transpose(idle[:, j, :], ident, ident)
@@ -171,11 +208,41 @@ def tile_staticgraphmodule_kernel(tc, x, Wp_words, Wp_scales, b, out):
         for i in range(1, len(banks)):
             flip(*banks[i])
             mean_pe(*banks[i - 1])
+            if i == 1:
+                flip1(4)
+            if i == 5:
+                flip1(0)
+                flip1(2)
+                for n in range(2):
+                    nc.sync.dma_start(out=xres[n][:], in_=x_mp[n])
         mean_pe(*banks[-1])
+        for j in range(5):
+            mean1(j)
         pb = psum.tile([P, 8, P], BF16, tag="bank", name="pb")
         nc.tensor.transpose(pb[:, 0, :], brow[:], ident)
         nc.scalar.copy(out=bias[:], in_=pb[:, 0, 0:4])
         nc.scalar.mul(out=negb[:], in_=pb[:, 0, 0:4], mul=-1.0)
+
+        tiles = [(0, m, c) for m in range(4) for c in range(2)] + [(1, m, c) for c in (1, 0) for m in range(4)]
+        accs = {}
+
+        def mx_pass(i, g):
+            n, m, c = tiles[i]
+            cs = slice(CH * c, CH * (c + 1))
+            codes, plane = ((xc[n], xs[n]), (mc[n], ms[n]))[g]
+            nc.tensor.matmul_mx(
+                out=accs[i][:],
+                lhsT=ww[:, g, 256 * m:256 * (m + 1)].bitcast(FP4X4),
+                lhsT_scale=wsc[:, g, P * m:P * (m + 1)],
+                rhs=codes[:, cs].bitcast(FP8X4),
+                rhs_scale=plane[:, cs],
+                start=(g == 0),
+                stop=(g == 1),
+            )
+
+        for i in range(AHEAD):
+            accs[i] = psum.tile([P, CH], F32, tag="bank", name="acc")
+            mx_pass(i, 0)
 
         nc.vector.quantize_mx(out=mc[0][:].bitcast(FP8X4), scales=ms[0][:], in_=gm[0][:].rearrange("p w t -> p (w t)"))
         for c in range(2):
@@ -189,23 +256,15 @@ def tile_staticgraphmodule_kernel(tc, x, Wp_words, Wp_scales, b, out):
                 op0=MULT, op1=ADD,
             )
 
-        tiles = [(0, m, c) for m in range(4) for c in range(2)] + [(1, m, c) for c in (1, 0) for m in range(4)]
         for i, (n, m, c) in enumerate(tiles):
             cs = slice(CH * c, CH * (c + 1))
             nc.scalar.activation(out=xb[n][:, m, cs], in_=xres[n][:, m, cs], func=IDENTITY, bias=bias[:, m:m + 1], scale=1.0)
-            acc = psum.tile([P, CH], F32, tag="bank", name="acc")
-            for g, codes, plane in ((0, xc[n], xs[n]), (1, mc[n], ms[n])):
-                nc.tensor.matmul_mx(
-                    out=acc[:],
-                    lhsT=ww[:, g, 256 * m:256 * (m + 1)].bitcast(FP4X4),
-                    lhsT_scale=wsc[:, g, P * m:P * (m + 1)],
-                    rhs=codes[:, cs].bitcast(FP8X4),
-                    rhs_scale=plane[:, cs],
-                    start=(g == 0),
-                    stop=(g == 1),
-                )
+            if i >= AHEAD:
+                accs[i] = psum.tile([P, CH], F32, tag="bank", name="acc")
+                mx_pass(i, 0)
+            mx_pass(i, 1)
             nc.vector.scalar_tensor_tensor(
-                out=xb[n][:, m, cs], in0=acc[:], scalar=negb[:, m:m + 1], in1=xb[n][:, m, cs], op0=MAX, op1=ADD
+                out=xb[n][:, m, cs], in0=accs[i][:], scalar=negb[:, m:m + 1], in1=xb[n][:, m, cs], op0=MAX, op1=ADD
             )
             nc.sync.dma_start(out=out_mp[n][:, m, cs], in_=xb[n][:, m, cs])
             if i == 6:

@@ -41,7 +41,7 @@ def tile_staticgraphmodule_kernel(tc, x, Wp_words, Wp_scales, b, out):
         out_mp = [out[n].rearrange("(m p) h w -> p m (h w)", p=P) for n in range(2)]
         xraw = [keep.tile([P, T, HW], BF16, name="xraw%d" % n) for n in range(2)]
         xres = [keep.tile([P, T, HW], BF16, name="xres%d" % n) for n in range(2)]
-        for n, r0, r1 in ((0, 0, 9), (1, 16, 24), (1, 24, 32), (0, 9, 17), (0, 17, 32), (1, 0, 16)):
+        for n, r0, r1 in ((0, 0, 5), (0, 5, 9), (1, 16, 24), (1, 24, 32), (0, 9, 17), (0, 17, 32), (1, 0, 16)):
             nc.sync.dma_start(out=xraw[n][:, :, SIDE * r0:SIDE * r1], in_=x_pj[n][:, :, SIDE * r0:SIDE * r1])
         ww = keep.tile([P, 2, 1024], U8, name="ww", align_bytes=64)
         nc.sync.dma_start(out=ww[:].bitcast(I32), in_=Wp_words.rearrange("g p c -> p g c").bitcast(I32))
@@ -68,8 +68,6 @@ def tile_staticgraphmodule_kernel(tc, x, Wp_words, Wp_scales, b, out):
         rz = keep.tile([P, 8, SIDE], BF16, name="rz")
         vz = keep.tile([P, 6, SIDE], BF16, name="vz")
         a_int = keep.tile([P, 6, SIDE], BF16, name="a_int")
-        a_first = keep.tile([P, 2 * SIDE], BF16, name="a_first")
-        a_last = keep.tile([P, 2 * SIDE], BF16, name="a_last")
         nc.vector.tensor_scalar_mul(out=z8[:], in0=z[:].rearrange("p (r w) -> p r w", w=SIDE), scalar1=0.125)
         vadd(hz[:, :, 1:31], z8[:, :, 0:30], z8[:, :, 2:32])
         vadd(hz[:, :, 0:32:31], z8[:, :, 0:31:30], z8[:, :, 1:32:30])
@@ -77,10 +75,10 @@ def tile_staticgraphmodule_kernel(tc, x, Wp_words, Wp_scales, b, out):
         vadd(vz[:], rz[:, 0:6, :], rz[:, 2:8, :])
         vadd(a_int[:], vz[:], hz[:, 1:7, :])
         af = a_int[:].rearrange("p r w -> p (r w)")
-        vadd(a_first[:, 0:32], af[:, 32:64], af[:, 0:32])
-        nc.vector.tensor_copy(out=a_first[:, 32:64], in_=af[:, 64:96])
+        vadd(af[:, 32:64], af[:, 32:64], af[:, 0:32])
         mid = af[:, 64:128]
-        a_top = keep.tile([P, 3 * SIDE], BF16, name="a_top")
+        a_top = af[:, 32:128]
+        a_last = af[:, 96:160]
 
         bias = keep.tile([P, 4], F32, name="bias")
         negb = keep.tile([P, 4], F32, name="negb")
@@ -136,7 +134,7 @@ def tile_staticgraphmodule_kernel(tc, x, Wp_words, Wp_scales, b, out):
             xt = xts[(n, a0)]
             done = 0
             for wi, (a, rows) in enumerate(windows(n, a0)):
-                band = a_first[:] if a == 0 else (a_last[:] if a == SIDE - 2 else af[:, 64:128])
+                band = a_top if a == 0 else (a_last if a == SIDE - 2 else mid)
                 for t in range(T):
                     nc.tensor.matmul(
                         out=pm[:, t, 64 * wi:64 * wi + SIDE * rows], lhsT=xt[:, T * wi + t, :], rhs=band[:, 0:SIDE * rows],
@@ -165,7 +163,7 @@ def tile_staticgraphmodule_kernel(tc, x, Wp_words, Wp_scales, b, out):
 
         def mean1(j):
             pm = psum.tile([P, T, P], F32, tag="bank", name="pm1")
-            parts = [(at, 0, a_top[:], 96)] if j == 0 else [(bt, j - 1, mid, 64), (at, j, mid, 64)]
+            parts = [(at, 0, a_top, 96)] if j == 0 else [(bt, j - 1, mid, 64), (at, j, mid, 64)]
             done = 0
             for xt, k, band, width in parts:
                 for t in range(T):
@@ -187,10 +185,7 @@ def tile_staticgraphmodule_kernel(tc, x, Wp_words, Wp_scales, b, out):
         regroup_x(0, 0, (1,))
         vadd(h4[:, lo:16, 0:32:31, :], x4[:, lo:16, 0:31:30, :], x4[:, lo:16, 1:32:30, :])
         vadd(hh[:, lo:16, T:ROW - T], x8[:, lo:16, 0:ROW - 2 * T], x8[:, lo:16, 2 * T:ROW])
-        nc.vector.tensor_copy(out=a_last[:, 0:32], in_=af[:, 96:128])
-        vadd(a_last[:, 32:64], af[:, 128:160], af[:, 160:192])
-        nc.vector.tensor_copy(out=a_top[:, 0:32], in_=a_first[:, 0:32])
-        nc.vector.tensor_copy(out=a_top[:, 32:96], in_=mid)
+        vadd(af[:, 128:160], af[:, 128:160], af[:, 160:192])
         regroup_x(0, 1)
         vadd(rr[:, lo:16, :], hh[:, lo:16, :], x8[:, lo:16, :])
         quantise(xg[0], xc[0], xs[0], 0)
@@ -216,7 +211,7 @@ def tile_staticgraphmodule_kernel(tc, x, Wp_words, Wp_scales, b, out):
                 for n in range(2):
                     nc.sync.dma_start(out=xres[n][:], in_=x_mp[n])
         mean_pe(*banks[-1])
-        for j in range(5):
+        for j in (4, 0, 1, 2, 3):
             mean1(j)
         pb = psum.tile([P, 8, P], BF16, tag="bank", name="pb")
         nc.tensor.transpose(pb[:, 0, :], brow[:], ident)
@@ -245,7 +240,7 @@ def tile_staticgraphmodule_kernel(tc, x, Wp_words, Wp_scales, b, out):
             mx_pass(i, 0)
 
         nc.vector.quantize_mx(out=mc[0][:].bitcast(FP8X4), scales=ms[0][:], in_=gm[0][:].rearrange("p w t -> p (w t)"))
-        for c in range(2):
+        for c in (1, 0):
             quantise(gm[1], mc[1], ms[1], c)
         one = keep.tile([P, 1], F32, name="one")
         nc.vector.memset(one[:], 1.0)

@@ -24,7 +24,7 @@ HW = SIDE * SIDE
 ROW = SIDE * T
 CH = 512
 PE_ROWS = (32, 19)
-AHEAD = 8
+AHEAD = 6
 V0 = PE_ROWS[1] - 16
 
 
@@ -191,9 +191,6 @@ def tile_staticgraphmodule_kernel(tc, x, Wp_words, Wp_scales, b, out):
         quantise(xg[0], xc[0], xs[0], 0)
         vadd(vv[:, V0:15, :], rr[:, V0 - 1:14, :], rr[:, V0 + 1:16, :])
         vadd(vv[:, 15:16, :], rr[:, 14:15, :], rr[:, 15:16, :])
-        quantise(xg[0], xc[0], xs[0], 1)
-        vadd(g1[:, V0:16, :], vv[:, V0:16, :], hh[:, V0:16, :])
-        quantise(xg[1], xc[1], xs[1], 1)
 
         banks = [(0, a0) for a0 in range(0, PE_ROWS[0], 4)]
         idle = psum.tile([P, 8, P], BF16, tag="bank", name="idle")
@@ -205,18 +202,21 @@ def tile_staticgraphmodule_kernel(tc, x, Wp_words, Wp_scales, b, out):
             mean_pe(*banks[i - 1])
             if i == 1:
                 flip1(4)
-            if i == 5:
+            if i == 4:
                 flip1(0)
                 flip1(2)
                 for n in range(2):
                     nc.sync.dma_start(out=xres[n][:], in_=x_mp[n])
+                pb = psum.tile([P, 8, P], BF16, tag="bank", name="pb")
+                nc.tensor.transpose(pb[:, 0, :], brow[:], ident)
+                nc.vector.tensor_copy(out=bias[:], in_=pb[:, 0, 0:4])
+                nc.vector.tensor_scalar_mul(out=negb[:], in0=pb[:, 0, 0:4], scalar1=-1.0)
+                quantise(xg[0], xc[0], xs[0], 1)
+                vadd(g1[:, V0:16, :], vv[:, V0:16, :], hh[:, V0:16, :])
+                quantise(xg[1], xc[1], xs[1], 1)
         mean_pe(*banks[-1])
         for j in (4, 0, 1, 2, 3):
             mean1(j)
-        pb = psum.tile([P, 8, P], BF16, tag="bank", name="pb")
-        nc.tensor.transpose(pb[:, 0, :], brow[:], ident)
-        nc.scalar.copy(out=bias[:], in_=pb[:, 0, 0:4])
-        nc.scalar.mul(out=negb[:], in_=pb[:, 0, 0:4], mul=-1.0)
 
         tiles = [(0, m, c) for m in range(4) for c in range(2)] + [(1, m, c) for c in (1, 0) for m in range(4)]
         accs = {}

from contextlib import ExitStack

import concourse.mybir as mybir
from concourse.masks import make_identity

FLOPS = 2 * 2 * 1024 * 512 * 1024

BF16 = mybir.dt.bfloat16
F32 = mybir.dt.float32
I32 = mybir.dt.int32
U8 = mybir.dt.uint8
U32 = mybir.dt.uint32
FP8X4 = mybir.dt.float8_e4m3fn_x4
FP4X4 = mybir.dt.float4_e2m1fn_x4
ADD = mybir.AluOpType.add
MAX = mybir.AluOpType.max
MULT = mybir.AluOpType.mult
IDENTITY = mybir.ActivationFunctionType.Identity

P = 128
T = 4
SIDE = 32
HW = SIDE * SIDE
ROW = SIDE * T
CH = 512
PE_ROWS = (32, 19)
AHEAD = 6
V0 = PE_ROWS[1] - 16


def tile_staticgraphmodule_kernel(tc, x, Wp_words, Wp_scales, b, out):
    nc = tc.nc
    with ExitStack() as ctx:
        keep = ctx.enter_context(tc.tile_pool(name="keep", bufs=1))
        xtpool = ctx.enter_context(tc.tile_pool(name="xtpool", bufs=4))
        psum = ctx.enter_context(tc.psum_pool(name="psum", bufs=8))
        ctx.enter_context(tc.manual_schedule())

        x_pj = [x[n].rearrange("(p j) h w -> p j (h w)", j=T) for n in range(2)]
        x_mp = [x[n].rearrange("(m p) h w -> p m (h w)", p=P) for n in range(2)]
        out_mp = [out[n].rearrange("(m p) h w -> p m (h w)", p=P) for n in range(2)]
        xraw = [keep.tile([P, T, HW], BF16, name="xraw%d" % n) for n in range(2)]
        xres = [keep.tile([P, T, HW], BF16, name="xres%d" % n) for n in range(2)]
        for n, r0, r1 in ((0, 0, 5), (0, 5, 9), (1, 16, 24), (1, 24, 32), (0, 9, 17), (0, 17, 32), (1, 0, 16)):
            nc.sync.dma_start(out=xraw[n][:, :, SIDE * r0:SIDE * r1], in_=x_pj[n][:, :, SIDE * r0:SIDE * r1])
        ww = keep.tile([P, 2, 1024], U8, name="ww", align_bytes=64)
        nc.sync.dma_start(out=ww[:].bitcast(I32), in_=Wp_words.rearrange("g p c -> p g c").bitcast(I32))
        wsc = keep.tile([P, 2, 512], U8, name="wsc", align_bytes=64)
        nc.vector.memset(wsc[:].bitcast(I32), 0)
        for q in range(4):
            nc.sync.dma_start(
                out=wsc[32 * q:32 * q + 4, :, :].bitcast(I32),
                in_=Wp_scales[:, 4 * q:4 * q + 4, :].rearrange("g r n -> r g n").bitcast(I32),
            )
        brow = keep.tile([P, P], BF16, name="brow")
        nc.vector.memset(brow[:].bitcast(I32), 0)
        nc.sync.dma_start(out=brow[0:4, :], in_=b.rearrange("(m p) -> m p", p=P))

        def vadd(o, a, c):
            nc.vector.tensor_tensor(out=o, in0=a, in1=c, op=ADD)

        z = keep.tile([P, 8 * SIDE], BF16, name="z")
        nc.gpsimd.memset(z[:], 0.0)
        make_identity(nc, z[:, 64:192], nomemset=True)
        ident = z[:, 64:192]
        z8 = keep.tile([P, 8, SIDE], BF16, name="z8")
        hz = keep.tile([P, 8, SIDE], BF16, name="hz")
        rz = keep.tile([P, 8, SIDE], BF16, name="rz")
        vz = keep.tile([P, 6, SIDE], BF16, name="vz")
        a_int = keep.tile([P, 6, SIDE], BF16, name="a_int")
        nc.vector.tensor_scalar_mul(out=z8[:], in0=z[:].rearrange("p (r w) -> p r w", w=SIDE), scalar1=0.125)
        vadd(hz[:, :, 1:31], z8[:, :, 0:30], z8[:, :, 2:32])
        vadd(hz[:, :, 0:32:31], z8[:, :, 0:31:30], z8[:, :, 1:32:30])
        vadd(rz[:], hz[:], z8[:])
        vadd(vz[:], rz[:, 0:6, :], rz[:, 2:8, :])
        vadd(a_int[:], vz[:], hz[:, 1:7, :])
        af = a_int[:].rearrange("p r w -> p (r w)")
        vadd(af[:, 32:64], af[:, 32:64], af[:, 0:32])
        mid = af[:, 64:128]
        a_top = af[:, 32:128]
        a_last = af[:, 96:160]

        bias = keep.tile([P, 4], F32, name="bias")
        negb = keep.tile([P, 4], F32, name="negb")
        xb = [keep.tile([P, 4, HW], F32, name="xb%d" % n) for n in range(2)]
        xg = [keep.tile([P, HW, T], BF16, name="xg%d" % n, align_bytes=64) for n in range(2)]
        gm = [keep.tile([P, HW, T], BF16, name="gm%d" % n, align_bytes=64) for n in range(2)]
        xc = [keep.tile([P, HW], U32, name="xc%d" % n, align_bytes=64) for n in range(2)]
        mc = [keep.tile([P, HW], U32, name="mc%d" % n, align_bytes=64) for n in range(2)]
        xs = [keep.tile([P, HW], U8, name="xs%d" % n, align_bytes=64) for n in range(2)]
        ms = [keep.tile([P, HW], U8, name="ms%d" % n, align_bytes=64) for n in range(2)]
        x8 = keep.tile([P, 16, ROW], BF16, name="x8")
        hh = keep.tile([P, 16, ROW], F32, name="hh")
        rr = keep.tile([P, 16, ROW], F32, name="rr")
        vv = keep.tile([P, 16, ROW], F32, name="vv")
        x4 = x8[:].rearrange("p i (j t) -> p i j t", t=T)
        h4 = hh[:].rearrange("p i (j t) -> p i j t", t=T)
        g1 = gm[1][:, CH:HW, :].rearrange("p (i j) t -> p i (j t)", j=SIDE)
        xts = {}
        at = keep.tile([P, 5, T * P], BF16, name="at")
        bt = keep.tile([P, 4, T * P], BF16, name="bt")

        def regroup_x(n, c, halves=(0, 1)):
            cs = slice(CH * c + 256 * halves[0], CH * c + 256 * (halves[-1] + 1))
            nc.vector.tensor_copy(out=xg[n][:, cs, :], in_=xraw[n][:, :, cs].rearrange("p t w -> p w t"))

        def quantise(src, codes, plane, c):
            cs = slice(CH * c, CH * (c + 1))
            nc.vector.quantize_mx(
                out=codes[:, cs].bitcast(FP8X4),
                scales=plane[:, cs],
                in_=src[:, cs, :].rearrange("p w t -> p (w t)"),
            )

        def windows(n, a0):
            return [(a, min(2, PE_ROWS[n] - a)) for a in (a0, a0 + 2) if a < PE_ROWS[n]]

        def flip(n, a0):
            pt = psum.tile([P, 8, P], BF16, tag="bank", name="pt")
            for wi, (a, rows) in enumerate(windows(n, a0)):
                first = min(max(a - 1, 0), SIDE - 4)
                for t in range(T):
                    nc.tensor.transpose(pt[:, T * wi + t, :], xraw[n][:, t, SIDE * first:SIDE * first + P], ident)
            xt = xtpool.tile([P, 8, P], BF16, tag="xt", name="xt")
            xts[(n, a0)] = xt
            used = T * len(windows(n, a0))
            nc.scalar.copy(
                out=xt[:, 0:used, :].rearrange("p a b -> p (a b)").bitcast(F32),
                in_=pt[:, 0:used, :].rearrange("p a b -> p (a b)").bitcast(F32),
            )

        def mean_pe(n, a0):
            pm = psum.tile([P, T, P], F32, tag="bank", name="pm")
            xt = xts[(n, a0)]
            done = 0
            for wi, (a, rows) in enumerate(windows(n, a0)):
                band = a_top if a == 0 else (a_last if a == SIDE - 2 else mid)
                for t in range(T):
                    nc.tensor.matmul(
                        out=pm[:, t, 64 * wi:64 * wi + SIDE * rows], lhsT=xt[:, T * wi + t, :], rhs=band[:, 0:SIDE * rows],
                        start=True, stop=True,
                    )
                done += SIDE * rows
            nc.scalar.copy(out=gm[n][:, SIDE * a0:SIDE * a0 + done, :], in_=pm[:, :, 0:done].rearrange("p t w -> p w t"))

        def flip1(k0):
            ks = [k for k in (k0, k0 + 1) if k < 5]
            pt = psum.tile([P, 8, P], BF16, tag="bank", name="pt1")
            for i, k in enumerate(ks):
                for t in range(T):
                    nc.tensor.transpose(pt[:, T * i + t, :], xraw[1][:, t, P * k:P * (k + 1)], ident)
            used = T * len(ks)
            nc.scalar.copy(
                out=at[:, k0:k0 + len(ks), :].rearrange("p a b -> p (a b)").bitcast(F32),
                in_=pt[:, 0:used, :].rearrange("p a b -> p (a b)").bitcast(F32),
            )
            up = [k for k in ks if k < 4]
            if up:
                nc.sync.dma_start(out=bt[0:64, up[0]:up[-1] + 1, :], in_=at[64:128, up[0]:up[-1] + 1, :])
            low = [k for k in ks if k >= 1]
            if low:
                nc.sync.dma_start(out=bt[64:128, low[0] - 1:low[-1], :], in_=at[0:64, low[0]:low[-1] + 1, :])

        def mean1(j):
            pm = psum.tile([P, T, P], F32, tag="bank", name="pm1")
            parts = [(at, 0, a_top, 96)] if j == 0 else [(bt, j - 1, mid, 64), (at, j, mid, 64)]
            done = 0
            for xt, k, band, width in parts:
                for t in range(T):
                    nc.tensor.matmul(
                        out=pm[:, t, done:done + width], lhsT=xt[:, k, P * t:P * (t + 1)], rhs=band[:, 0:width],
                        start=True, stop=True,
                    )
                done += width
            first = SIDE * max(4 * j - 1, 0)
            nc.scalar.copy(out=gm[1][:, first:first + done, :], in_=pm[:, :, 0:done].rearrange("p t w -> p w t"))

        lo = V0 - 1
        x1 = xg[1][:, CH:HW, :].rearrange("p (i j) t -> p i (j t)", j=SIDE)
        regroup_x(0, 0, (0,))
        regroup_x(1, 1, (0,))
        regroup_x(1, 1, (1,))
        nc.vector.tensor_scalar_mul(out=x8[:, lo:8, :], in0=x1[:, lo:8, :], scalar1=0.125)
        nc.vector.tensor_scalar_mul(out=x8[:, 8:16, :], in0=x1[:, 8:16, :], scalar1=0.125)
        regroup_x(0, 0, (1,))
        vadd(h4[:, lo:16, 0:32:31, :], x4[:, lo:16, 0:31:30, :], x4[:, lo:16, 1:32:30, :])
        vadd(hh[:, lo:16, T:ROW - T], x8[:, lo:16, 0:ROW - 2 * T], x8[:, lo:16, 2 * T:ROW])
        vadd(af[:, 128:160], af[:, 128:160], af[:, 160:192])
        regroup_x(0, 1)
        vadd(rr[:, lo:16, :], hh[:, lo:16, :], x8[:, lo:16, :])
        quantise(xg[0], xc[0], xs[0], 0)
        vadd(vv[:, V0:15, :], rr[:, V0 - 1:14, :], rr[:, V0 + 1:16, :])
        vadd(vv[:, 15:16, :], rr[:, 14:15, :], rr[:, 15:16, :])

        banks = [(0, a0) for a0 in range(0, PE_ROWS[0], 4)]
        idle = psum.tile([P, 8, P], BF16, tag="bank", name="idle")
        for j in range(8):
            nc.tensor.transpose(idle[:, j, :], ident, ident)
        flip(*banks[0])
        for i in range(1, len(banks)):
            flip(*banks[i])
            mean_pe(*banks[i - 1])
            if i == 1:
                flip1(4)
            if i == 4:
                flip1(0)
                flip1(2)
                for n in range(2):
                    nc.sync.dma_start(out=xres[n][:], in_=x_mp[n])
                pb = psum.tile([P, 8, P], BF16, tag="bank", name="pb")
                nc.tensor.transpose(pb[:, 0, :], brow[:], ident)
                nc.vector.tensor_copy(out=bias[:], in_=pb[:, 0, 0:4])
                nc.vector.tensor_scalar_mul(out=negb[:], in0=pb[:, 0, 0:4], scalar1=-1.0)
                quantise(xg[0], xc[0], xs[0], 1)
                vadd(g1[:, V0:16, :], vv[:, V0:16, :], hh[:, V0:16, :])
                quantise(xg[1], xc[1], xs[1], 1)
        mean_pe(*banks[-1])
        for j in (4, 0, 1, 2, 3):
            mean1(j)

        tiles = [(0, m, c) for m in range(4) for c in range(2)] + [(1, m, c) for c in (1, 0) for m in range(4)]
        accs = {}

        def mx_pass(i, g):
            n, m, c = tiles[i]
            cs = slice(CH * c, CH * (c + 1))
            codes, plane = ((xc[n], xs[n]), (mc[n], ms[n]))[g]
            nc.tensor.matmul_mx(
                out=accs[i][:],
                lhsT=ww[:, g, 256 * m:256 * (m + 1)].bitcast(FP4X4),
                lhsT_scale=wsc[:, g, P * m:P * (m + 1)],
                rhs=codes[:, cs].bitcast(FP8X4),
                rhs_scale=plane[:, cs],
                start=(g == 0),
                stop=(g == 1),
            )

        for i in range(AHEAD):
            accs[i] = psum.tile([P, CH], F32, tag="bank", name="acc")
            mx_pass(i, 0)

        nc.vector.quantize_mx(out=mc[0][:].bitcast(FP8X4), scales=ms[0][:], in_=gm[0][:].rearrange("p w t -> p (w t)"))
        for c in (1, 0):
            quantise(gm[1], mc[1], ms[1], c)
        one = keep.tile([P, 1], F32, name="one")
        nc.vector.memset(one[:], 1.0)
        for q in range(4):
            qs = slice(P * q, P * (q + 1))
            nc.gpsimd.tensor_scalar(
                out=xg[1][:, qs, :], in0=xraw[1][:, :, qs].rearrange("p t w -> p w t"), scalar1=one[:, 0:1], scalar2=0.0,
                op0=MULT, op1=ADD,
            )

        for i, (n, m, c) in enumerate(tiles):
            cs = slice(CH * c, CH * (c + 1))
            nc.scalar.activation(out=xb[n][:, m, cs], in_=xres[n][:, m, cs], func=IDENTITY, bias=bias[:, m:m + 1], scale=1.0)
            if i >= AHEAD:
                accs[i] = psum.tile([P, CH], F32, tag="bank", name="acc")
                mx_pass(i, 0)
            mx_pass(i, 1)
            nc.vector.scalar_tensor_tensor(
                out=xb[n][:, m, cs], in0=accs[i][:], scalar=negb[:, m:m + 1], in1=xb[n][:, m, cs], op0=MAX, op1=ADD
            )
            nc.sync.dma_start(out=out_mp[n][:, m, cs], in_=xb[n][:, m, cs])
            if i == 6:
                quantise(xg[1], xc[1], xs[1], 0)
